import numpy as np
import ml_dtypes


def mxq(x, axis, fmt="e4m3"):
    dtype, down = {"e4m3": (ml_dtypes.float8_e4m3fn, 7), "e5m2": (ml_dtypes.float8_e5m2, 14)}[fmt]
    v = np.moveaxis(np.asarray(x, np.float32).astype(ml_dtypes.bfloat16).astype(np.float64), axis, -1)
    blocks = v.reshape(v.shape[:-1] + (-1, 32))
    amax = np.abs(blocks).max(-1, keepdims=True)
    byte = np.maximum(np.where(amax > 0, np.frexp(amax)[1] - 1 + 127, 0) - down, 1)
    scale = np.exp2(byte - 127.0)
    codes = (blocks / scale).astype(np.float32).astype(dtype).astype(np.float64)
    return np.moveaxis((codes * scale).reshape(v.shape), -1, axis)


WIDE = False


def mx_kscale(k):
    if not WIDE:
        return np.ones(k)
    levels = np.array([10, -10, 5, -5, 0])
    if k % 512:
        return np.exp2(np.random.permutation(np.resize(levels, k // 32))).repeat(32)
    a = np.empty((k // 512, 16))
    for p in range(k // 512):
        a[p, :8] = np.random.permutation(np.resize(levels, 8))
        for g in range(8):
            far = levels[np.abs(levels - a[p, g]) >= 10]
            a[p, g + 8] = far[np.random.randint(len(far))]
    return np.exp2(a.ravel()).repeat(32)


BF16 = ml_dtypes.bfloat16


def bf(x):
    return np.asarray(x, np.float32).astype(BF16)


def f64(x):
    return np.asarray(x).astype(np.float64)


B, S, DIM, N_HEADS, Q_LORA, KV_LORA, NOPE, ROPE, V_HEAD = 4, 1024, 1024, 2, 512, 512, 128, 64, 128
QK_HEAD = NOPE + ROPE
EPS = 1e-6


def rmsnorm(v, w):
    return v * (1.0 / np.sqrt(np.mean(v * v, axis=-1, keepdims=True) + EPS)) * w


def apply_rope(v, cos, sin):
    vr = v.reshape(v.shape[:-1] + (-1, 2))
    c = cos[None, :, None, :]
    s = sin[None, :, None, :]
    re = vr[..., 0] * c - vr[..., 1] * s
    im = vr[..., 0] * s + vr[..., 1] * c
    return np.stack([re, im], axis=-1).reshape(v.shape)


def setup_inputs():
    s, t = mx_kscale(DIM), mx_kscale(Q_LORA)
    inv_freq = 1.0 / (10000.0 ** (np.arange(0, ROPE, 2) / ROPE))
    ang = np.arange(S)[:, None] * inv_freq[None, :]
    return {"x": bf(np.random.standard_normal((B, S, DIM)) * s),
            "freqs_cos": bf(np.cos(ang)),
            "freqs_sin": bf(np.sin(ang)),
            "wq_a": bf(np.random.standard_normal((Q_LORA, DIM)) / np.sqrt(DIM) / s),
            "q_norm_w": bf((1.0 + 0.1 * np.random.standard_normal(Q_LORA)) * t),
            "wq_b": bf(np.random.standard_normal((N_HEADS * QK_HEAD, Q_LORA)) / np.sqrt(Q_LORA) / t)}


def reference(x, freqs_cos, freqs_sin, wq_a, q_norm_w, wq_b):
    ql = mxq(f64(x), 2, "e4m3") @ mxq(f64(wq_a), 1, "e4m3").T
    qn = rmsnorm(ql, f64(q_norm_w))
    q = mxq(qn, 2, "e4m3") @ mxq(f64(wq_b), 1, "e4m3").T
    q = q.reshape(B, S, N_HEADS, QK_HEAD)
    q_nope = np.ascontiguousarray(q[..., :NOPE])
    q_pe = apply_rope(q[..., NOPE:], f64(freqs_cos), f64(freqs_sin))
    return q_nope, q_pe

@@ -1,0 +1,379 @@
+from contextlib import ExitStack
+
+import concourse.mybir as mybir
+from concourse.masks import make_identity
+
+F32 = mybir.dt.float32
+BF16 = mybir.dt.bfloat16
+U32 = mybir.dt.uint32
+U8 = mybir.dt.uint8
+FP8X4 = mybir.dt.float8_e4m3fn_x4
+ACT = mybir.ActivationFunctionType
+ALU = mybir.AluOpType
+
+P = 128
+PACK = 4
+K_PASS = P * PACK
+
+BATCH, SEQ, DIM = 4, 1024, 1024
+Q_LORA = 512
+HEADS, NOPE, ROPE = 2, 128, 64
+EPS = 1e-6
+
+SEQ_TILES = SEQ // P
+PASSES_1 = DIM // K_PASS
+WORD_BLOCKS = DIM // 2 // P
+NOPE_COLS = HEADS * NOPE
+ROPE_COLS = HEADS * ROPE
+Q_COLS = NOPE_COLS + 2 * ROPE_COLS
+
+ROUND_TILES = 2
+ROUNDS = BATCH * SEQ_TILES // ROUND_TILES
+ROUNDS_PER_BATCH = SEQ_TILES // ROUND_TILES
+
+PRODUCT_1_LAG = 1
+NORMALISE_LAG = 2
+TURN_QN_LAG = 3
+PRODUCT_2_LAG = 4
+FINISH_LAG = 5
+PREPARE_WQ_A_STEP = 0
+PREPARE_ROTATION_STEP = 1
+PREPARE_WQ_B_STEP = 2
+
+FLOPS = 2 * BATCH * SEQ * (DIM * Q_LORA + Q_LORA * HEADS * (NOPE + ROPE))
+
+
+def tile_mla_pa_t_kernel(
+    tc, x, freqs_cos, freqs_sin, wq_a, q_norm_w, wq_b, out_0, out_1
+):
+    nc = tc.nc
+
+    x_view = x.rearrange("b (p s) k -> b p s k", s=SEQ_TILES)
+    nope_view = out_0.rearrange("b (p s) h d -> b p s (h d)", s=SEQ_TILES)
+    rope_view = out_1.rearrange("b (p s) h d -> b p s (h d)", s=SEQ_TILES)
+
+    with ExitStack() as ctx:
+        ctx.enter_context(tc.manual_schedule())
+
+        keep = ctx.enter_context(tc.tile_pool(name="keep", bufs=1))
+        pair = ctx.enter_context(tc.tile_pool(name="pair", bufs=2))
+        ring = ctx.enter_context(tc.tile_pool(name="ring", bufs=3))
+        ps_words = ctx.enter_context(tc.psum_pool(name="ps_words", bufs=2))
+        ps_ql = ctx.enter_context(tc.psum_pool(name="ps_ql", bufs=3))
+        ps_qnt = ctx.enter_context(tc.psum_pool(name="ps_qnt", bufs=1))
+        ps_nope = ctx.enter_context(tc.psum_pool(name="ps_nope", bufs=1))
+        ps_rope = ctx.enter_context(tc.psum_pool(name="ps_rope", bufs=1))
+
+        def copy_out(index, out, in_):
+            if index % 2 == 0:
+                nc.scalar.copy(out=out, in_=in_)
+            else:
+                nc.vector.tensor_copy(out=out, in_=in_)
+
+        x_rows = []
+        for rnd in range(ROUNDS):
+            x_round = keep.tile([P, ROUND_TILES, DIM], BF16, name="x_round%d" % rnd)
+            x_rows.append(x_round)
+
+        def load_x(rnd):
+            b, s0 = rnd // ROUNDS_PER_BATCH, (rnd % ROUNDS_PER_BATCH) * ROUND_TILES
+            nc.sync.dma_start(out=x_rows[rnd][:], in_=x_view[b, :, s0 : s0 + ROUND_TILES, :])
+
+        load_x(0)
+
+        wa_rows = keep.tile([P, PACK, DIM], BF16)
+        wa_view = wq_a.rearrange("(r t) k -> r t k", t=PACK)
+        for t in range(0, PACK, 2):
+            nc.sync.dma_start(out=wa_rows[:, t : t + 2, :], in_=wa_view[:, t : t + 2, :])
+
+        load_x(1)
+
+        wb_rows = keep.tile([P, HEADS + 1, Q_LORA], BF16)
+        wb_heads = wq_b.rearrange("(h d) k -> d h k", h=HEADS)
+        nc.sync.dma_start(out=wb_rows[:, 0:HEADS, :], in_=wb_heads[0:NOPE, :, :])
+        for h in range(HEADS):
+            nc.sync.dma_start(
+                out=wb_rows[h * ROPE : (h + 1) * ROPE, HEADS, :],
+                in_=wb_heads[NOPE : NOPE + ROPE, h, :],
+            )
+        for rnd in range(2, ROUNDS):
+            load_x(rnd)
+
+        gain_row = keep.tile([P, Q_LORA], BF16)
+        nc.gpsimd.memset(gain_row[:], 0.0)
+        nc.scalar.dma_start(out=gain_row[0:1, :], in_=q_norm_w.rearrange("(o n) -> o n", o=1))
+        cos_rows = keep.tile([P, SEQ_TILES, ROPE // 2], BF16)
+        sin_rows = keep.tile([P, SEQ_TILES, ROPE // 2], BF16)
+        nc.scalar.dma_start(
+            out=cos_rows[:], in_=freqs_cos.rearrange("(p s) f -> p s f", s=SEQ_TILES)
+        )
+        nc.scalar.dma_start(
+            out=sin_rows[:], in_=freqs_sin.rearrange("(p s) f -> p s f", s=SEQ_TILES)
+        )
+
+        ident_f32 = keep.tile([P, P], F32)
+        make_identity(nc, ident_f32[:])
+        ident_bf16 = keep.tile([P, P], BF16)
+        make_identity(nc, ident_bf16[:])
+        ones = keep.tile([P, P], BF16)
+        nc.gpsimd.memset(ones[:], 1.0)
+
+        warm = keep.tile([P, 1], F32)
+        nc.scalar.activation(out=warm[:], in_=ones[:, 0:1], func=ACT.Abs_reciprocal_sqrt)
+
+        rot = keep.tile([P, SEQ_TILES, 2, ROPE], F32)
+
+        def prepare_rotation():
+            rot_pairs = rot[:].rearrange("p s c (f e) -> p s c f e", e=2)
+            nc.vector.tensor_copy(
+                out=rot_pairs[:, :, 0, :, :],
+                in_=cos_rows[:].unsqueeze(3).to_broadcast([P, SEQ_TILES, ROPE // 2, 2]),
+            )
+            nc.vector.tensor_scalar_mul(
+                out=rot_pairs[:, :, 1, :, 0], in0=sin_rows[:], scalar1=-1.0
+            )
+            nc.vector.tensor_copy(out=rot_pairs[:, :, 1, :, 1], in_=sin_rows[:])
+
+        def idle_bank(which, blocks):
+            pool, tag = (
+                (ps_qnt, "qnt"),
+                (ps_nope, "nope_bank"),
+                (ps_rope, "rope_bank"),
+                (ps_ql, "ql"),
+            )[which]
+            return pool.tile([P, blocks, P], F32, tag=tag, name="weight_bank")
+
+        def turn_words(bank, word_blocks):
+            for slot, block in enumerate(word_blocks):
+                nc.tensor.transpose(bank[:, slot, :], block, ident_f32[:])
+
+        def blocks_of_row_words(words):
+            return [
+                words[:, 2 * P * g + u : 2 * P * (g + 1) : 2]
+                for g in range(PASSES_1)
+                for u in range(2)
+            ]
+
+        wa_codes = keep.tile([P, PASSES_1, Q_LORA], U32, align_bytes=64)
+        wa_scales = keep.tile([P, PASSES_1, Q_LORA], U8, align_bytes=64)
+        gain = keep.tile([P, Q_LORA], F32)
+
+        def prepare_wq_a():
+            grouped = keep.tile([P, PASSES_1 * Q_LORA * PACK], BF16, align_bytes=64, name="wa_grouped")
+            grouped_words = grouped[:].bitcast(F32).rearrange(
+                "p (g n u) -> p g n u", g=PASSES_1, u=2
+            )
+            for t in range(PACK):
+                bank = idle_bank(t, WORD_BLOCKS)
+                turn_words(bank, blocks_of_row_words(wa_rows[:, t, :].bitcast(F32)))
+                copy_out(
+                    t,
+                    out=grouped_words[:, :, t * P : (t + 1) * P, :],
+                    in_=bank[:].rearrange("p (g u) r -> p g r u", u=2),
+                )
+                if t % 2 == 1:
+                    cols = slice((t - 1) * P, (t + 1) * P)
+                    for g in range(PASSES_1):
+                        first = (g * Q_LORA + (t - 1) * P) * PACK
+                        nc.vector.quantize_mx(
+                            out=wa_codes[:, g, cols].bitcast(FP8X4),
+                            scales=wa_scales[:, g, cols],
+                            in_=grouped[:, first : first + 2 * P * PACK],
+                        )
+            spread = ps_ql.tile([P, Q_LORA], F32, tag="ql")
+            nc.tensor.matmul(out=spread[:], lhsT=ones[:], rhs=gain_row[:], start=True, stop=True)
+            nc.scalar.copy(
+                out=gain[:].rearrange("p (t r) -> p t r", t=PACK),
+                in_=spread[:].rearrange("p (r t) -> p t r", t=PACK),
+            )
+
+        wb_codes = keep.tile([P, Q_COLS], U32, align_bytes=64)
+        wb_scales = keep.tile([P, Q_COLS], U8, align_bytes=64)
+
+        def prepare_wq_b():
+            grouped = keep.tile([P, Q_COLS * PACK], BF16, align_bytes=64, name="wb_grouped")
+            grouped_words = grouped[:].bitcast(F32).rearrange("p (n u) -> p n u", u=2)
+
+            def every_second_word(i):
+                words = wb_rows[:, i, :].bitcast(F32).rearrange("r (p u) -> r u p", u=2)
+                return [words[:, u, :] for u in range(2)]
+
+            bank = idle_bank(1, 2 * HEADS)
+            turn_words(bank, every_second_word(0) + every_second_word(1))
+            nc.scalar.copy(
+                out=grouped_words[:, 0:NOPE_COLS, :].rearrange("p (i r) u -> p i r u", i=HEADS),
+                in_=bank[:].rearrange("p (i u) r -> p i r u", u=2),
+            )
+            bank = idle_bank(2, 2)
+            turn_words(bank, every_second_word(HEADS))
+            nc.scalar.copy(
+                out=grouped_words[:, NOPE_COLS : NOPE_COLS + ROPE_COLS, :],
+                in_=bank[:].rearrange("p u r -> p r u"),
+            )
+            swapped = grouped_words[:, NOPE_COLS + ROPE_COLS : Q_COLS, :].rearrange(
+                "p (m e) u -> p m e u", e=2
+            )
+            row_pairs = bank[:].rearrange("p u (m e) -> p m e u", e=2)
+            for e in range(2):
+                nc.scalar.copy(out=swapped[:, :, 1 - e, :], in_=row_pairs[:, :, e, :])
+            nc.vector.quantize_mx(
+                out=wb_codes[:].bitcast(FP8X4), scales=wb_scales[:], in_=grouped[:]
+            )
+
+        x_grouped, x_mx, ql_banks, rstd_of = {}, {}, {}, {}
+        qn_of, qn_grouped, qn_mx, q_banks = {}, {}, {}, {}
+
+        def turn_x(rnd):
+            grouped = pair.tile([P, ROUND_TILES * DIM], BF16, align_bytes=64, tag="x_grouped")
+            grouped_words = grouped[:].bitcast(F32).rearrange(
+                "p (j g r u) -> p j g r u", j=ROUND_TILES, g=PASSES_1, u=2
+            )
+            for j in range(ROUND_TILES):
+                bank = ps_words.tile([P, WORD_BLOCKS, P], F32, tag="words")
+                turn_words(bank, blocks_of_row_words(x_rows[rnd][:, j, :].bitcast(F32)))
+                copy_out(
+                    j, out=grouped_words[:, j], in_=bank[:].rearrange("p (g u) r -> p g r u", u=2)
+                )
+            x_grouped[rnd] = grouped
+
+        def quantise_x(rnd):
+            codes = ring.tile([P, ROUND_TILES * PASSES_1 * P], U32, align_bytes=64, tag="x_codes")
+            scales = ring.tile([P, ROUND_TILES * PASSES_1 * P], U8, align_bytes=64, tag="x_scales")
+            nc.vector.quantize_mx(
+                out=codes[:].bitcast(FP8X4), scales=scales[:], in_=x_grouped[rnd][:]
+            )
+            x_mx[rnd] = (codes, scales)
+
+        def product_1(rnd):
+            codes, scales = x_mx[rnd]
+            sum_sq = ring.tile([P, ROUND_TILES], F32, tag="sum_sq")
+            ql_banks[rnd] = []
+            for j in range(ROUND_TILES):
+                ql = ps_ql.tile([P, Q_LORA], F32, tag="ql")
+                for g in range(PASSES_1):
+                    tok = slice((j * PASSES_1 + g) * P, (j * PASSES_1 + g + 1) * P)
+                    nc.tensor.matmul_mx(
+                        out=ql[:],
+                        lhsT=codes[:, tok].bitcast(FP8X4),
+                        lhsT_scale=scales[:, tok],
+                        rhs=wa_codes[:, g, :].bitcast(FP8X4),
+                        rhs_scale=wa_scales[:, g, :],
+                        start=(g == 0),
+                        stop=(g == PASSES_1 - 1),
+                    )
+                squares = pair.tile([P, Q_LORA], BF16, tag="squares")
+                nc.scalar.activation(
+                    out=squares[:], in_=ql[:], func=ACT.Square, accum_out=sum_sq[:, j : j + 1]
+                )
+                ql_banks[rnd].append(ql)
+            rstd = ring.tile([P, ROUND_TILES], F32, tag="rstd")
+            nc.scalar.activation(
+                out=rstd[:],
+                in_=sum_sq[:],
+                func=ACT.Abs_reciprocal_sqrt,
+                bias=EPS,
+                scale=1.0 / Q_LORA,
+            )
+            rstd_of[rnd] = rstd
+
+        def normalise(rnd):
+            rstd = rstd_of[rnd]
+            qn = ring.tile([P, ROUND_TILES, Q_LORA], BF16, tag="qn")
+            for j in range(ROUND_TILES):
+                nc.vector.scalar_tensor_tensor(
+                    out=qn[:, j, :],
+                    in0=ql_banks[rnd][j][:],
+                    scalar=rstd[:, j : j + 1],
+                    in1=gain[:],
+                    op0=ALU.mult,
+                    op1=ALU.mult,
+                )
+            qn_of[rnd] = qn
+
+        def turn_qn(rnd):
+            qnt = ps_qnt.tile([P, ROUND_TILES, PACK, P], BF16, tag="qnt")
+            for j in range(ROUND_TILES):
+                for t in range(PACK):
+                    nc.tensor.transpose(
+                        qnt[:, j, t, :], qn_of[rnd][:, j, t * P : (t + 1) * P], ident_bf16[:]
+                    )
+            grouped = pair.tile([P, ROUND_TILES * Q_LORA], BF16, align_bytes=64, tag="qn_grouped")
+            nc.scalar.copy(
+                out=grouped[:].rearrange("p (j r t) -> p j r t", j=ROUND_TILES, t=PACK),
+                in_=qnt[:].rearrange("p j t r -> p j r t"),
+            )
+            qn_grouped[rnd] = grouped
+
+        def quantise_qn(rnd):
+            codes = ring.tile([P, ROUND_TILES * P], U32, align_bytes=64, tag="qn_codes")
+            scales = ring.tile([P, ROUND_TILES * P], U8, align_bytes=64, tag="qn_scales")
+            nc.vector.quantize_mx(
+                out=codes[:].bitcast(FP8X4), scales=scales[:], in_=qn_grouped[rnd][:]
+            )
+            qn_mx[rnd] = (codes, scales)
+
+        def product_2(rnd):
+            codes, scales = qn_mx[rnd]
+            nope_bank = ps_nope.tile([P, ROUND_TILES, NOPE_COLS], F32, tag="nope_bank")
+            rope_bank = ps_rope.tile([P, ROUND_TILES, 2 * ROPE_COLS], F32, tag="rope_bank")
+            for j in range(ROUND_TILES):
+                tok = slice(j * P, (j + 1) * P)
+                for bank, cols in (
+                    (nope_bank, slice(0, NOPE_COLS)),
+                    (rope_bank, slice(NOPE_COLS, Q_COLS)),
+                ):
+                    nc.tensor.matmul_mx(
+                        out=bank[:, j, :],
+                        lhsT=codes[:, tok].bitcast(FP8X4),
+                        lhsT_scale=scales[:, tok],
+                        rhs=wb_codes[:, cols].bitcast(FP8X4),
+                        rhs_scale=wb_scales[:, cols],
+                        start=True,
+                        stop=True,
+                    )
+            q_banks[rnd] = (nope_bank, rope_bank)
+
+        def finish(rnd):
+            b, s0 = rnd // ROUNDS_PER_BATCH, (rnd % ROUNDS_PER_BATCH) * ROUND_TILES
+            nope_bank, rope_bank = q_banks[rnd]
+            nope = ring.tile([P, ROUND_TILES, NOPE_COLS], F32, tag="nope")
+            nc.scalar.copy(out=nope[:], in_=nope_bank[:])
+            terms = ring.tile([P, ROUND_TILES, 2 * ROPE_COLS], F32, tag="terms")
+            nc.vector.tensor_tensor(
+                out=terms[:].rearrange("p j (c h d) -> p (j c) h d", c=2, h=HEADS),
+                in0=rope_bank[:].rearrange("p j (c h d) -> p (j c) h d", c=2, h=HEADS),
+                in1=rot[:, s0 : s0 + ROUND_TILES]
+                .rearrange("p s c d -> p (s c) d")
+                .unsqueeze(2)
+                .to_broadcast([P, 2 * ROUND_TILES, HEADS, ROPE]),
+                op=ALU.mult,
+            )
+            rope = ring.tile([P, ROUND_TILES, ROPE_COLS], F32, tag="rope")
+            nc.gpsimd.tensor_tensor(
+                out=rope[:],
+                in0=terms[:, :, 0:ROPE_COLS],
+                in1=terms[:, :, ROPE_COLS : 2 * ROPE_COLS],
+                op=ALU.add,
+            )
+            nc.sync.dma_start(out=nope_view[b, :, s0 : s0 + ROUND_TILES, :], in_=nope[:])
+            nc.sync.dma_start(out=rope_view[b, :, s0 : s0 + ROUND_TILES, :], in_=rope[:])
+
+        def run(stage_of_round, rnd):
+            if 0 <= rnd < ROUNDS:
+                stage_of_round(rnd)
+
+        for step in range(ROUNDS + FINISH_LAG):
+            run(finish, step - FINISH_LAG)
+            run(normalise, step - NORMALISE_LAG)
+            run(turn_x, step)
+            run(turn_qn, step - TURN_QN_LAG)
+            run(quantise_qn, step - TURN_QN_LAG)
+            run(quantise_x, step)
+            if step == PREPARE_WQ_A_STEP:
+                prepare_wq_a()
+            if step == PREPARE_ROTATION_STEP:
+                prepare_rotation()
+            if step == PREPARE_WQ_B_STEP:
+                prepare_wq_b()
+            run(product_1, step - PRODUCT_1_LAG)
+            run(product_2, step - PRODUCT_2_LAG)

@@ -113,8 +113,6 @@ def tile_mla_pa_t_kernel(
 
         ident_f32 = keep.tile([P, P], F32)
         make_identity(nc, ident_f32[:])
-        ident_bf16 = keep.tile([P, P], BF16)
-        make_identity(nc, ident_bf16[:])
         ones = keep.tile([P, P], BF16)
         nc.gpsimd.memset(ones[:], 1.0)
 
@@ -163,28 +161,32 @@ def tile_mla_pa_t_kernel(
             grouped_words = grouped[:].bitcast(F32).rearrange(
                 "p (g n u) -> p g n u", g=PASSES_1, u=2
             )
-            for t in range(PACK):
-                bank = idle_bank(t, WORD_BLOCKS)
-                turn_words(bank, blocks_of_row_words(wa_rows[:, t, :].bitcast(F32)))
-                copy_out(
-                    t,
-                    out=grouped_words[:, :, t * P : (t + 1) * P, :],
-                    in_=bank[:].rearrange("p (g u) r -> p g r u", u=2),
-                )
-                if t % 2 == 1:
-                    cols = slice((t - 1) * P, (t + 1) * P)
-                    for g in range(PASSES_1):
-                        first = (g * Q_LORA + (t - 1) * P) * PACK
-                        nc.vector.quantize_mx(
-                            out=wa_codes[:, g, cols].bitcast(FP8X4),
-                            scales=wa_scales[:, g, cols],
-                            in_=grouped[:, first : first + 2 * P * PACK],
-                        )
+            for v in range(2):
+                cols = slice(v * 2 * P, (v + 1) * 2 * P)
+                for g in range(PASSES_1):
+                    bank = idle_bank(v * PASSES_1 + g, WORD_BLOCKS)
+                    blocks = []
+                    for e in range(2):
+                        row_blocks = blocks_of_row_words(wa_rows[:, 2 * v + e, :].bitcast(F32))
+                        blocks += row_blocks[2 * g : 2 * g + 2]
+                    turn_words(bank, blocks)
+                    copy_out(
+                        g,
+                        out=grouped_words[:, g, cols, :].rearrange("p (r e) u -> p r e u", e=2),
+                        in_=bank[:].rearrange("p (e u) r -> p r e u", u=2),
+                    )
+                for g in range(PASSES_1):
+                    first = (g * Q_LORA + v * 2 * P) * PACK
+                    nc.vector.quantize_mx(
+                        out=wa_codes[:, g, cols].bitcast(FP8X4),
+                        scales=wa_scales[:, g, cols],
+                        in_=grouped[:, first : first + 2 * P * PACK],
+                    )
             spread = ps_ql.tile([P, Q_LORA], F32, tag="ql")
             nc.tensor.matmul(out=spread[:], lhsT=ones[:], rhs=gain_row[:], start=True, stop=True)
             nc.scalar.copy(
-                out=gain[:].rearrange("p (t r) -> p t r", t=PACK),
-                in_=spread[:].rearrange("p (r t) -> p t r", t=PACK),
+                out=gain[:].rearrange("p (v r e) -> p v r e", v=2, e=2),
+                in_=spread[:].rearrange("p (r v e) -> p v r e", v=2, e=2),
             )
 
         wb_codes = keep.tile([P, Q_COLS], U32, align_bytes=64)
@@ -291,16 +293,16 @@ def tile_mla_pa_t_kernel(
             qn_of[rnd] = qn
 
         def turn_qn(rnd):
-            qnt = ps_qnt.tile([P, ROUND_TILES, PACK, P], BF16, tag="qnt")
+            qnt = ps_qnt.tile([P, ROUND_TILES * 2, P], F32, tag="qnt")
+            blocks = []
             for j in range(ROUND_TILES):
-                for t in range(PACK):
-                    nc.tensor.transpose(
-                        qnt[:, j, t, :], qn_of[rnd][:, j, t * P : (t + 1) * P], ident_bf16[:]
-                    )
+                words = qn_of[rnd][:, j, :].bitcast(F32)
+                blocks += [words[:, v * P : (v + 1) * P] for v in range(2)]
+            turn_words(qnt, blocks)
             grouped = pair.tile([P, ROUND_TILES * Q_LORA], BF16, align_bytes=64, tag="qn_grouped")
             nc.scalar.copy(
-                out=grouped[:].rearrange("p (j r t) -> p j r t", j=ROUND_TILES, t=PACK),
-                in_=qnt[:].rearrange("p j t r -> p j r t"),
+                out=grouped[:].bitcast(F32).rearrange("p (j r v) -> p j r v", j=ROUND_TILES, v=2),
+                in_=qnt[:].rearrange("p (j v) r -> p j r v", v=2),
             )
             qn_grouped[rnd] = grouped
 

@@ -30,14 +30,13 @@ Q_COLS = NOPE_COLS + 2 * ROPE_COLS
 ROUND_TILES = 2
 ROUNDS = BATCH * SEQ_TILES // ROUND_TILES
 ROUNDS_PER_BATCH = SEQ_TILES // ROUND_TILES
+LAST = ROUNDS - 1
 
 PRODUCT_1_LAG = 1
 NORMALISE_LAG = 2
 TURN_QN_LAG = 3
 PRODUCT_2_LAG = 4
 FINISH_LAG = 5
-PREPARE_WQ_A_STEP = 0
-PREPARE_ROTATION_STEP = 1
 PREPARE_WQ_B_STEP = 2
 
 FLOPS = 2 * BATCH * SEQ * (DIM * Q_LORA + Q_LORA * HEADS * (NOPE + ROPE))
@@ -75,18 +74,27 @@ def tile_mla_pa_t_kernel(
             x_round = keep.tile([P, ROUND_TILES, DIM], BF16, name="x_round%d" % rnd)
             x_rows.append(x_round)
 
-        def load_x(rnd):
+        def load_x(rnd, tiles=slice(0, ROUND_TILES)):
             b, s0 = rnd // ROUNDS_PER_BATCH, (rnd % ROUNDS_PER_BATCH) * ROUND_TILES
-            nc.sync.dma_start(out=x_rows[rnd][:], in_=x_view[b, :, s0 : s0 + ROUND_TILES, :])
-
-        load_x(0)
+            nc.sync.dma_start(
+                out=x_rows[rnd][:, tiles, :],
+                in_=x_view[b, :, s0 + tiles.start : s0 + tiles.stop, :],
+            )
 
         wa_rows = keep.tile([P, PACK, DIM], BF16)
         wa_view = wq_a.rearrange("(r t) k -> r t k", t=PACK)
-        for t in range(0, PACK, 2):
-            nc.sync.dma_start(out=wa_rows[:, t : t + 2, :], in_=wa_view[:, t : t + 2, :])
 
+        def load_wq_a(t):
+            nc.sync.dma_start(out=wa_rows[:, t, :], in_=wa_view[:, t, :])
+
+        load_x(0, slice(0, 1))
+        load_wq_a(0)
+        load_wq_a(1)
+        load_x(0, slice(1, 2))
+        load_wq_a(2)
+        load_wq_a(3)
         load_x(1)
+        load_x(2)
 
         wb_rows = keep.tile([P, HEADS + 1, Q_LORA], BF16)
         wb_heads = wq_b.rearrange("(h d) k -> d h k", h=HEADS)
@@ -96,41 +104,33 @@ def tile_mla_pa_t_kernel(
                 out=wb_rows[h * ROPE : (h + 1) * ROPE, HEADS, :],
                 in_=wb_heads[NOPE : NOPE + ROPE, h, :],
             )
-        for rnd in range(2, ROUNDS):
+        for rnd in range(3, ROUNDS):
             load_x(rnd)
 
         gain_row = keep.tile([P, Q_LORA], BF16)
         nc.gpsimd.memset(gain_row[:], 0.0)
         nc.scalar.dma_start(out=gain_row[0:1, :], in_=q_norm_w.rearrange("(o n) -> o n", o=1))
-        cos_rows = keep.tile([P, SEQ_TILES, ROPE // 2], BF16)
-        sin_rows = keep.tile([P, SEQ_TILES, ROPE // 2], BF16)
-        nc.scalar.dma_start(
-            out=cos_rows[:], in_=freqs_cos.rearrange("(p s) f -> p s f", s=SEQ_TILES)
-        )
-        nc.scalar.dma_start(
-            out=sin_rows[:], in_=freqs_sin.rearrange("(p s) f -> p s f", s=SEQ_TILES)
-        )
+        freqs_rows = keep.tile([P, 2, SEQ_TILES, ROPE // 2], BF16)
+        for c, freqs in enumerate((freqs_cos, freqs_sin)):
+            nc.scalar.dma_start(
+                out=freqs_rows[:, c], in_=freqs.rearrange("(p s) f -> p s f", s=SEQ_TILES)
+            )
 
         ident_f32 = keep.tile([P, P], F32)
         make_identity(nc, ident_f32[:])
         ones = keep.tile([P, P], BF16)
         nc.gpsimd.memset(ones[:], 1.0)
 
+        rot = keep.tile([P, SEQ_TILES, 2, ROPE], BF16)
+
+        def prepare_rotation(c):
+            nc.vector.tensor_copy(
+                out=rot[:, :, c, :].rearrange("p s (f e) -> p s f e", e=2),
+                in_=freqs_rows[:, c].unsqueeze(3).to_broadcast([P, SEQ_TILES, ROPE // 2, 2]),
+            )
+
         warm = keep.tile([P, 1], F32)
         nc.scalar.activation(out=warm[:], in_=ones[:, 0:1], func=ACT.Abs_reciprocal_sqrt)
-
-        rot = keep.tile([P, SEQ_TILES, 2, ROPE], F32)
-
-        def prepare_rotation():
-            rot_pairs = rot[:].rearrange("p s c (f e) -> p s c f e", e=2)
-            nc.vector.tensor_copy(
-                out=rot_pairs[:, :, 0, :, :],
-                in_=cos_rows[:].unsqueeze(3).to_broadcast([P, SEQ_TILES, ROPE // 2, 2]),
-            )
-            nc.vector.tensor_scalar_mul(
-                out=rot_pairs[:, :, 1, :, 0], in0=sin_rows[:], scalar1=-1.0
-            )
-            nc.vector.tensor_copy(out=rot_pairs[:, :, 1, :, 1], in_=sin_rows[:])
 
         def idle_bank(which, blocks):
             pool, tag = (
@@ -156,32 +156,39 @@ def tile_mla_pa_t_kernel(
         wa_scales = keep.tile([P, PASSES_1, Q_LORA], U8, align_bytes=64)
         gain = keep.tile([P, Q_LORA], F32)
 
-        def prepare_wq_a():
-            grouped = keep.tile([P, PASSES_1 * Q_LORA * PACK], BF16, align_bytes=64, name="wa_grouped")
-            grouped_words = grouped[:].bitcast(F32).rearrange(
+        wa_grouped = keep.tile([P, PASSES_1 * Q_LORA * PACK], BF16, align_bytes=64)
+
+        def turn_wq_a(v):
+            banks = [idle_bank(v * PASSES_1 + g, WORD_BLOCKS) for g in range(PASSES_1)]
+            for e in range(2):
+                blocks = blocks_of_row_words(wa_rows[:, 2 * v + e, :].bitcast(F32))
+                for g in range(PASSES_1):
+                    for u in range(2):
+                        nc.tensor.transpose(
+                            banks[g][:, 2 * e + u, :], blocks[2 * g + u], ident_f32[:]
+                        )
+            return banks
+
+        def copy_wq_a(v, g, bank, copy):
+            cols = slice(v * 2 * P, (v + 1) * 2 * P)
+            grouped_words = wa_grouped[:].bitcast(F32).rearrange(
                 "p (g n u) -> p g n u", g=PASSES_1, u=2
             )
-            for v in range(2):
-                cols = slice(v * 2 * P, (v + 1) * 2 * P)
-                for g in range(PASSES_1):
-                    bank = idle_bank(v * PASSES_1 + g, WORD_BLOCKS)
-                    blocks = []
-                    for e in range(2):
-                        row_blocks = blocks_of_row_words(wa_rows[:, 2 * v + e, :].bitcast(F32))
-                        blocks += row_blocks[2 * g : 2 * g + 2]
-                    turn_words(bank, blocks)
-                    copy_out(
-                        g,
-                        out=grouped_words[:, g, cols, :].rearrange("p (r e) u -> p r e u", e=2),
-                        in_=bank[:].rearrange("p (e u) r -> p r e u", u=2),
-                    )
-                for g in range(PASSES_1):
-                    first = (g * Q_LORA + v * 2 * P) * PACK
-                    nc.vector.quantize_mx(
-                        out=wa_codes[:, g, cols].bitcast(FP8X4),
-                        scales=wa_scales[:, g, cols],
-                        in_=grouped[:, first : first + 2 * P * PACK],
-                    )
+            copy(
+                out=grouped_words[:, g, cols, :].rearrange("p (r e) u -> p r e u", e=2),
+                in_=bank[:].rearrange("p (e u) r -> p r e u", u=2),
+            )
+
+        def quantise_wq_a(v, g):
+            cols = slice(v * 2 * P, (v + 1) * 2 * P)
+            first = (g * Q_LORA + v * 2 * P) * PACK
+            nc.vector.quantize_mx(
+                out=wa_codes[:, g, cols].bitcast(FP8X4),
+                scales=wa_scales[:, g, cols],
+                in_=wa_grouped[:, first : first + 2 * P * PACK],
+            )
+
+        def spread_gain():
             spread = ps_ql.tile([P, Q_LORA], F32, tag="ql")
             nc.tensor.matmul(out=spread[:], lhsT=ones[:], rhs=gain_row[:], start=True, stop=True)
             nc.scalar.copy(
@@ -192,8 +199,10 @@ def tile_mla_pa_t_kernel(
         wb_codes = keep.tile([P, Q_COLS], U32, align_bytes=64)
         wb_scales = keep.tile([P, Q_COLS], U8, align_bytes=64)
 
+        wb_grouped = keep.tile([P, Q_COLS * PACK], BF16, align_bytes=64)
+
         def prepare_wq_b():
-            grouped = keep.tile([P, Q_COLS * PACK], BF16, align_bytes=64, name="wb_grouped")
+            grouped = wb_grouped
             grouped_words = grouped[:].bitcast(F32).rearrange("p (n u) -> p n u", u=2)
 
             def every_second_word(i):
@@ -202,7 +211,7 @@ def tile_mla_pa_t_kernel(
 
             bank = idle_bank(1, 2 * HEADS)
             turn_words(bank, every_second_word(0) + every_second_word(1))
-            nc.scalar.copy(
+            nc.vector.tensor_copy(
                 out=grouped_words[:, 0:NOPE_COLS, :].rearrange("p (i r) u -> p i r u", i=HEADS),
                 in_=bank[:].rearrange("p (i u) r -> p i r u", u=2),
             )
@@ -212,31 +221,42 @@ def tile_mla_pa_t_kernel(
                 out=grouped_words[:, NOPE_COLS : NOPE_COLS + ROPE_COLS, :],
                 in_=bank[:].rearrange("p u r -> p r u"),
             )
-            swapped = grouped_words[:, NOPE_COLS + ROPE_COLS : Q_COLS, :].rearrange(
-                "p (m e) u -> p m e u", e=2
+            first = (NOPE_COLS + ROPE_COLS) * PACK
+            row_pairs = grouped[:, NOPE_COLS * PACK : first].rearrange(
+                "p (m e t) -> p m e t", e=2, t=PACK
             )
-            row_pairs = bank[:].rearrange("p u (m e) -> p m e u", e=2)
-            for e in range(2):
-                nc.scalar.copy(out=swapped[:, :, 1 - e, :], in_=row_pairs[:, :, e, :])
+            swapped = grouped[:, first:].rearrange("p (m e t) -> p m e t", e=2, t=PACK)
+            nc.vector.tensor_scalar_mul(
+                out=swapped[:, :, 0, :], in0=row_pairs[:, :, 1, :], scalar1=-1.0
+            )
+            nc.vector.tensor_copy(out=swapped[:, :, 1, :], in_=row_pairs[:, :, 0, :])
+
+        def quantise_wq_b():
             nc.vector.quantize_mx(
-                out=wb_codes[:].bitcast(FP8X4), scales=wb_scales[:], in_=grouped[:]
+                out=wb_codes[:].bitcast(FP8X4), scales=wb_scales[:], in_=wb_grouped[:]
             )
 
-        x_grouped, x_mx, ql_banks, rstd_of = {}, {}, {}, {}
-        qn_of, qn_grouped, qn_mx, q_banks = {}, {}, {}, {}
+        x_banks, x_grouped, x_mx, ql_banks, rstd_of = {}, {}, {}, {}, {}
+        qn_of, qn_banks, qn_grouped, qn_mx, q_banks = {}, {}, {}, {}, {}
 
-        def turn_x(rnd):
-            grouped = pair.tile([P, ROUND_TILES * DIM], BF16, align_bytes=64, tag="x_grouped")
-            grouped_words = grouped[:].bitcast(F32).rearrange(
+        def turn_x(rnd, j):
+            if j == 0:
+                grouped = pair.tile([P, ROUND_TILES * DIM], BF16, align_bytes=64, tag="x_grouped")
+                x_grouped[rnd] = grouped
+                x_banks[rnd] = []
+            bank = ps_words.tile([P, WORD_BLOCKS, P], F32, tag="words")
+            turn_words(bank, blocks_of_row_words(x_rows[rnd][:, j, :].bitcast(F32)))
+            x_banks[rnd].append(bank)
+
+        def copy_x(rnd, j):
+            grouped_words = x_grouped[rnd][:].bitcast(F32).rearrange(
                 "p (j g r u) -> p j g r u", j=ROUND_TILES, g=PASSES_1, u=2
             )
-            for j in range(ROUND_TILES):
-                bank = ps_words.tile([P, WORD_BLOCKS, P], F32, tag="words")
-                turn_words(bank, blocks_of_row_words(x_rows[rnd][:, j, :].bitcast(F32)))
-                copy_out(
-                    j, out=grouped_words[:, j], in_=bank[:].rearrange("p (g u) r -> p g r u", u=2)
-                )
-            x_grouped[rnd] = grouped
+            copy_out(
+                j,
+                out=grouped_words[:, j],
+                in_=x_banks[rnd][j][:].rearrange("p (g u) r -> p g r u", u=2),
+            )
 
         def quantise_x(rnd):
             codes = ring.tile([P, ROUND_TILES * PASSES_1 * P], U32, align_bytes=64, tag="x_codes")
@@ -248,7 +268,6 @@ def tile_mla_pa_t_kernel(
 
         def product_1(rnd):
             codes, scales = x_mx[rnd]
-            sum_sq = ring.tile([P, ROUND_TILES], F32, tag="sum_sq")
             ql_banks[rnd] = []
             for j in range(ROUND_TILES):
                 ql = ps_ql.tile([P, Q_LORA], F32, tag="ql")
@@ -263,19 +282,28 @@ def tile_mla_pa_t_kernel(
                         start=(g == 0),
                         stop=(g == PASSES_1 - 1),
                     )
+                ql_banks[rnd].append(ql)
+
+        def root_mean_square(rnd):
+            sum_sq = ring.tile([P, ROUND_TILES], F32, tag="sum_sq")
+            rstd = ring.tile([P, ROUND_TILES], F32, tag="rstd")
+            root_tiles = 1 if rnd == LAST else ROUND_TILES
+            for j in range(ROUND_TILES):
                 squares = pair.tile([P, Q_LORA], BF16, tag="squares")
                 nc.scalar.activation(
-                    out=squares[:], in_=ql[:], func=ACT.Square, accum_out=sum_sq[:, j : j + 1]
+                    out=squares[:],
+                    in_=ql_banks[rnd][j][:],
+                    func=ACT.Square,
+                    accum_out=sum_sq[:, j : j + 1],
                 )
-                ql_banks[rnd].append(ql)
-            rstd = ring.tile([P, ROUND_TILES], F32, tag="rstd")
-            nc.scalar.activation(
-                out=rstd[:],
-                in_=sum_sq[:],
-                func=ACT.Abs_reciprocal_sqrt,
-                bias=EPS,
-                scale=1.0 / Q_LORA,
-            )
+                if (j + 1) % root_tiles == 0:
+                    nc.scalar.activation(
+                        out=rstd[:, j + 1 - root_tiles : j + 1],
+                        in_=sum_sq[:, j + 1 - root_tiles : j + 1],
+                        func=ACT.Abs_reciprocal_sqrt,
+                        bias=EPS,
+                        scale=1.0 / Q_LORA,
+                    )
             rstd_of[rnd] = rstd
 
         def normalise(rnd):
@@ -299,10 +327,13 @@ def tile_mla_pa_t_kernel(
                 words = qn_of[rnd][:, j, :].bitcast(F32)
                 blocks += [words[:, v * P : (v + 1) * P] for v in range(2)]
             turn_words(qnt, blocks)
+            qn_banks[rnd] = qnt
+
+        def copy_qn(rnd):
             grouped = pair.tile([P, ROUND_TILES * Q_LORA], BF16, align_bytes=64, tag="qn_grouped")
             nc.scalar.copy(
                 out=grouped[:].bitcast(F32).rearrange("p (j r v) -> p j r v", j=ROUND_TILES, v=2),
-                in_=qnt[:].rearrange("p (j v) r -> p j r v", v=2),
+                in_=qn_banks[rnd][:].rearrange("p (j v) r -> p j r v", v=2),
             )
             qn_grouped[rnd] = grouped
 
@@ -316,14 +347,17 @@ def tile_mla_pa_t_kernel(
 
         def product_2(rnd):
             codes, scales = qn_mx[rnd]
-            nope_bank = ps_nope.tile([P, ROUND_TILES, NOPE_COLS], F32, tag="nope_bank")
-            rope_bank = ps_rope.tile([P, ROUND_TILES, 2 * ROPE_COLS], F32, tag="rope_bank")
-            for j in range(ROUND_TILES):
-                tok = slice(j * P, (j + 1) * P)
-                for bank, cols in (
-                    (nope_bank, slice(0, NOPE_COLS)),
-                    (rope_bank, slice(NOPE_COLS, Q_COLS)),
-                ):
+            spare = rnd in (LAST - 2, LAST)
+            pool, tag = (ps_words, "words") if spare else (ps_nope, "nope_bank")
+            nope_bank = pool.tile([P, ROUND_TILES, NOPE_COLS], F32, tag=tag, name="nope_bank")
+            pool, tag = (ps_words, "words") if spare else (ps_rope, "rope_bank")
+            rope_bank = pool.tile([P, ROUND_TILES, 2 * ROPE_COLS], F32, tag=tag, name="rope_bank")
+            for bank, cols in (
+                (rope_bank, slice(NOPE_COLS, Q_COLS)),
+                (nope_bank, slice(0, NOPE_COLS)),
+            ):
+                for j in range(ROUND_TILES):
+                    tok = slice(j * P, (j + 1) * P)
                     nc.tensor.matmul_mx(
                         out=bank[:, j, :],
                         lhsT=codes[:, tok].bitcast(FP8X4),
@@ -335,11 +369,18 @@ def tile_mla_pa_t_kernel(
                     )
             q_banks[rnd] = (nope_bank, rope_bank)
 
-        def finish(rnd):
-            b, s0 = rnd // ROUNDS_PER_BATCH, (rnd % ROUNDS_PER_BATCH) * ROUND_TILES
-            nope_bank, rope_bank = q_banks[rnd]
+        def place(rnd):
+            return rnd // ROUNDS_PER_BATCH, (rnd % ROUNDS_PER_BATCH) * ROUND_TILES
+
+        def copy_nope(rnd):
+            b, s0 = place(rnd)
             nope = ring.tile([P, ROUND_TILES, NOPE_COLS], F32, tag="nope")
-            nc.scalar.copy(out=nope[:], in_=nope_bank[:])
+            nc.scalar.copy(out=nope[:], in_=q_banks[rnd][0][:])
+            nc.sync.dma_start(out=nope_view[b, :, s0 : s0 + ROUND_TILES, :], in_=nope[:])
+
+        def rotate(rnd):
+            b, s0 = place(rnd)
+            rope_bank = q_banks[rnd][1]
             terms = ring.tile([P, ROUND_TILES, 2 * ROPE_COLS], F32, tag="terms")
             nc.vector.tensor_tensor(
                 out=terms[:].rearrange("p j (c h d) -> p (j c) h d", c=2, h=HEADS),
@@ -351,31 +392,73 @@ def tile_mla_pa_t_kernel(
                 op=ALU.mult,
             )
             rope = ring.tile([P, ROUND_TILES, ROPE_COLS], F32, tag="rope")
-            nc.gpsimd.tensor_tensor(
+            adder = nc.vector if rnd == LAST else nc.gpsimd
+            adder.tensor_tensor(
                 out=rope[:],
                 in0=terms[:, :, 0:ROPE_COLS],
                 in1=terms[:, :, ROPE_COLS : 2 * ROPE_COLS],
                 op=ALU.add,
             )
-            nc.sync.dma_start(out=nope_view[b, :, s0 : s0 + ROUND_TILES, :], in_=nope[:])
             nc.sync.dma_start(out=rope_view[b, :, s0 : s0 + ROUND_TILES, :], in_=rope[:])
 
         def run(stage_of_round, rnd):
             if 0 <= rnd < ROUNDS:
                 stage_of_round(rnd)
 
-        for step in range(ROUNDS + FINISH_LAG):
-            run(finish, step - FINISH_LAG)
+        turn_x(0, 0)
+        copy_x(0, 0)
+        banks = turn_wq_a(0)
+        copy_wq_a(0, 0, banks[0], nc.vector.tensor_copy)
+        copy_wq_a(0, 1, banks[1], nc.scalar.copy)
+        turn_x(0, 1)
+        quantise_wq_a(0, 0)
+        quantise_wq_a(0, 1)
+        copy_x(0, 1)
+        banks = turn_wq_a(1)
+        copy_wq_a(1, 0, banks[0], nc.scalar.copy)
+        copy_wq_a(1, 1, banks[1], nc.scalar.copy)
+        quantise_x(0)
+        quantise_wq_a(1, 0)
+        quantise_wq_a(1, 1)
+        spread_gain()
+
+        for step in range(1, ROUNDS + 1):
+            run(copy_nope, step - FINISH_LAG)
+            run(rotate, step - FINISH_LAG)
+            if step - FINISH_LAG in (-2, -1):
+                prepare_rotation(step - FINISH_LAG + 2)
             run(normalise, step - NORMALISE_LAG)
-            run(turn_x, step)
+            if step < ROUNDS:
+                for j in range(ROUND_TILES):
+                    turn_x(step, j)
+                    copy_x(step, j)
             run(turn_qn, step - TURN_QN_LAG)
+            run(copy_qn, step - TURN_QN_LAG)
             run(quantise_qn, step - TURN_QN_LAG)
             run(quantise_x, step)
-            if step == PREPARE_WQ_A_STEP:
-                prepare_wq_a()
-            if step == PREPARE_ROTATION_STEP:
-                prepare_rotation()
+            if step == PREPARE_WQ_B_STEP + 1:
+                quantise_wq_b()
+            run(product_1, step - PRODUCT_1_LAG)
+            run(root_mean_square, step - PRODUCT_1_LAG)
+            run(product_2, step - PRODUCT_2_LAG)
             if step == PREPARE_WQ_B_STEP:
                 prepare_wq_b()
-            run(product_1, step - PRODUCT_1_LAG)
-            run(product_2, step - PRODUCT_2_LAG)
+
+        normalise(LAST)
+        turn_qn(LAST - 1)
+        copy_qn(LAST - 1)
+        copy_nope(LAST - 3)
+        rotate(LAST - 3)
+        quantise_qn(LAST - 1)
+        product_2(LAST - 2)
+        turn_qn(LAST)
+        copy_qn(LAST)
+        copy_nope(LAST - 2)
+        rotate(LAST - 2)
+        quantise_qn(LAST)
+        product_2(LAST - 1)
+        copy_nope(LAST - 1)
+        rotate(LAST - 1)
+        product_2(LAST)
+        copy_nope(LAST)
+        rotate(LAST)

@@ -121,7 +121,7 @@ def tile_mla_pa_t_kernel(
         ones = keep.tile([P, P], BF16)
         nc.gpsimd.memset(ones[:], 1.0)
 
-        rot = keep.tile([P, SEQ_TILES, 2, ROPE], BF16)
+        rot = keep.tile([P, SEQ_TILES, 2, ROPE], F32)
 
         def prepare_rotation(c):
             nc.vector.tensor_copy(

@@ -57,6 +57,7 @@ def tile_mla_pa_t_kernel(
         keep = ctx.enter_context(tc.tile_pool(name="keep", bufs=1))
         pair = ctx.enter_context(tc.tile_pool(name="pair", bufs=2))
         ring = ctx.enter_context(tc.tile_pool(name="ring", bufs=3))
+        once = ctx.enter_context(tc.tile_pool(name="once", bufs=ROUNDS))
         ps_words = ctx.enter_context(tc.psum_pool(name="ps_words", bufs=2))
         ps_ql = ctx.enter_context(tc.psum_pool(name="ps_ql", bufs=3))
         ps_qnt = ctx.enter_context(tc.psum_pool(name="ps_qnt", bufs=1))
@@ -124,7 +125,7 @@ def tile_mla_pa_t_kernel(
         rot = keep.tile([P, SEQ_TILES, 2, ROPE], F32)
 
         def prepare_rotation(c):
-            nc.vector.tensor_copy(
+            nc.scalar.copy(
                 out=rot[:, :, c, :].rearrange("p s (f e) -> p s f e", e=2),
                 in_=freqs_rows[:, c].unsqueeze(3).to_broadcast([P, SEQ_TILES, ROPE // 2, 2]),
             )
@@ -211,7 +212,7 @@ def tile_mla_pa_t_kernel(
 
             bank = idle_bank(1, 2 * HEADS)
             turn_words(bank, every_second_word(0) + every_second_word(1))
-            nc.vector.tensor_copy(
+            nc.scalar.copy(
                 out=grouped_words[:, 0:NOPE_COLS, :].rearrange("p (i r) u -> p i r u", i=HEADS),
                 in_=bank[:].rearrange("p (i u) r -> p i r u", u=2),
             )
@@ -221,11 +222,13 @@ def tile_mla_pa_t_kernel(
                 out=grouped_words[:, NOPE_COLS : NOPE_COLS + ROPE_COLS, :],
                 in_=bank[:].rearrange("p u r -> p r u"),
             )
+
+        def exchange_wq_b():
             first = (NOPE_COLS + ROPE_COLS) * PACK
-            row_pairs = grouped[:, NOPE_COLS * PACK : first].rearrange(
+            row_pairs = wb_grouped[:, NOPE_COLS * PACK : first].rearrange(
                 "p (m e t) -> p m e t", e=2, t=PACK
             )
-            swapped = grouped[:, first:].rearrange("p (m e t) -> p m e t", e=2, t=PACK)
+            swapped = wb_grouped[:, first:].rearrange("p (m e t) -> p m e t", e=2, t=PACK)
             nc.vector.tensor_scalar_mul(
                 out=swapped[:, :, 0, :], in0=row_pairs[:, :, 1, :], scalar1=-1.0
             )
@@ -285,8 +288,8 @@ def tile_mla_pa_t_kernel(
                 ql_banks[rnd].append(ql)
 
         def root_mean_square(rnd):
-            sum_sq = ring.tile([P, ROUND_TILES], F32, tag="sum_sq")
-            rstd = ring.tile([P, ROUND_TILES], F32, tag="rstd")
+            sum_sq = once.tile([P, ROUND_TILES], F32, tag="sum_sq")
+            rstd = once.tile([P, ROUND_TILES], F32, tag="rstd")
             root_tiles = 1 if rnd == LAST else ROUND_TILES
             for j in range(ROUND_TILES):
                 squares = pair.tile([P, Q_LORA], BF16, tag="squares")
@@ -338,8 +341,8 @@ def tile_mla_pa_t_kernel(
             qn_grouped[rnd] = grouped
 
         def quantise_qn(rnd):
-            codes = ring.tile([P, ROUND_TILES * P], U32, align_bytes=64, tag="qn_codes")
-            scales = ring.tile([P, ROUND_TILES * P], U8, align_bytes=64, tag="qn_scales")
+            codes = once.tile([P, ROUND_TILES * P], U32, align_bytes=64, tag="qn_codes")
+            scales = once.tile([P, ROUND_TILES * P], U8, align_bytes=64, tag="qn_scales")
             nc.vector.quantize_mx(
                 out=codes[:].bitcast(FP8X4), scales=scales[:], in_=qn_grouped[rnd][:]
             )
@@ -374,14 +377,14 @@ def tile_mla_pa_t_kernel(
 
         def copy_nope(rnd):
             b, s0 = place(rnd)
-            nope = ring.tile([P, ROUND_TILES, NOPE_COLS], F32, tag="nope")
+            nope = once.tile([P, ROUND_TILES, NOPE_COLS], F32, tag="nope")
             nc.scalar.copy(out=nope[:], in_=q_banks[rnd][0][:])
             nc.sync.dma_start(out=nope_view[b, :, s0 : s0 + ROUND_TILES, :], in_=nope[:])
 
         def rotate(rnd):
             b, s0 = place(rnd)
             rope_bank = q_banks[rnd][1]
-            terms = ring.tile([P, ROUND_TILES, 2 * ROPE_COLS], F32, tag="terms")
+            terms = once.tile([P, ROUND_TILES, 2 * ROPE_COLS], F32, tag="terms")
             nc.vector.tensor_tensor(
                 out=terms[:].rearrange("p j (c h d) -> p (j c) h d", c=2, h=HEADS),
                 in0=rope_bank[:].rearrange("p j (c h d) -> p (j c) h d", c=2, h=HEADS),
@@ -391,7 +394,7 @@ def tile_mla_pa_t_kernel(
                 .to_broadcast([P, 2 * ROUND_TILES, HEADS, ROPE]),
                 op=ALU.mult,
             )
-            rope = ring.tile([P, ROUND_TILES, ROPE_COLS], F32, tag="rope")
+            rope = once.tile([P, ROUND_TILES, ROPE_COLS], F32, tag="rope")
             adder = nc.vector if rnd == LAST else nc.gpsimd
             adder.tensor_tensor(
                 out=rope[:],
@@ -428,6 +431,8 @@ def tile_mla_pa_t_kernel(
             if step - FINISH_LAG in (-2, -1):
                 prepare_rotation(step - FINISH_LAG + 2)
             run(normalise, step - NORMALISE_LAG)
+            if step == PREPARE_WQ_B_STEP + 1:
+                exchange_wq_b()
             if step < ROUNDS:
                 for j in range(ROUND_TILES):
                     turn_x(step, j)

@@ -153,11 +153,11 @@ def tile_mla_pa_t_kernel(
                 for u in range(2)
             ]
 
-        wa_codes = keep.tile([P, PASSES_1, Q_LORA], U32, align_bytes=64)
-        wa_scales = keep.tile([P, PASSES_1, Q_LORA], U8, align_bytes=64)
+        wa_codes = keep.tile([P, PASSES_1, Q_LORA], U32, align_bytes=256)
+        wa_scales = keep.tile([P, PASSES_1, Q_LORA], U8, align_bytes=256)
         gain = keep.tile([P, Q_LORA], F32)
 
-        wa_grouped = keep.tile([P, PASSES_1 * Q_LORA * PACK], BF16, align_bytes=64)
+        wa_grouped = keep.tile([P, PASSES_1 * Q_LORA * PACK], BF16, align_bytes=256)
 
         def turn_wq_a(v):
             banks = [idle_bank(v * PASSES_1 + g, WORD_BLOCKS) for g in range(PASSES_1)]
@@ -197,10 +197,10 @@ def tile_mla_pa_t_kernel(
                 in_=spread[:].rearrange("p (r v e) -> p v r e", v=2, e=2),
             )
 
-        wb_codes = keep.tile([P, Q_COLS], U32, align_bytes=64)
-        wb_scales = keep.tile([P, Q_COLS], U8, align_bytes=64)
+        wb_codes = keep.tile([P, Q_COLS], U32, align_bytes=256)
+        wb_scales = keep.tile([P, Q_COLS], U8, align_bytes=256)
 
-        wb_grouped = keep.tile([P, Q_COLS * PACK], BF16, align_bytes=64)
+        wb_grouped = keep.tile([P, Q_COLS * PACK], BF16, align_bytes=256)
 
         def prepare_wq_b():
             grouped = wb_grouped
@@ -244,7 +244,7 @@ def tile_mla_pa_t_kernel(
 
         def turn_x(rnd, j):
             if j == 0:
-                grouped = pair.tile([P, ROUND_TILES * DIM], BF16, align_bytes=64, tag="x_grouped")
+                grouped = pair.tile([P, ROUND_TILES * DIM], BF16, align_bytes=256, tag="x_grouped")
                 x_grouped[rnd] = grouped
                 x_banks[rnd] = []
             bank = ps_words.tile([P, WORD_BLOCKS, P], F32, tag="words")
@@ -262,8 +262,8 @@ def tile_mla_pa_t_kernel(
             )
 
         def quantise_x(rnd):
-            codes = ring.tile([P, ROUND_TILES * PASSES_1 * P], U32, align_bytes=64, tag="x_codes")
-            scales = ring.tile([P, ROUND_TILES * PASSES_1 * P], U8, align_bytes=64, tag="x_scales")
+            codes = ring.tile([P, ROUND_TILES * PASSES_1 * P], U32, align_bytes=256, tag="x_codes")
+            scales = ring.tile([P, ROUND_TILES * PASSES_1 * P], U8, align_bytes=256, tag="x_scales")
             nc.vector.quantize_mx(
                 out=codes[:].bitcast(FP8X4), scales=scales[:], in_=x_grouped[rnd][:]
             )
@@ -333,7 +333,7 @@ def tile_mla_pa_t_kernel(
             qn_banks[rnd] = qnt
 
         def copy_qn(rnd):
-            grouped = pair.tile([P, ROUND_TILES * Q_LORA], BF16, align_bytes=64, tag="qn_grouped")
+            grouped = pair.tile([P, ROUND_TILES * Q_LORA], BF16, align_bytes=256, tag="qn_grouped")
             nc.scalar.copy(
                 out=grouped[:].bitcast(F32).rearrange("p (j r v) -> p j r v", j=ROUND_TILES, v=2),
                 in_=qn_banks[rnd][:].rearrange("p (j v) r -> p j r v", v=2),
@@ -341,8 +341,8 @@ def tile_mla_pa_t_kernel(
             qn_grouped[rnd] = grouped
 
         def quantise_qn(rnd):
-            codes = once.tile([P, ROUND_TILES * P], U32, align_bytes=64, tag="qn_codes")
-            scales = once.tile([P, ROUND_TILES * P], U8, align_bytes=64, tag="qn_scales")
+            codes = once.tile([P, ROUND_TILES * P], U32, align_bytes=256, tag="qn_codes")
+            scales = once.tile([P, ROUND_TILES * P], U8, align_bytes=256, tag="qn_scales")
             nc.vector.quantize_mx(
                 out=codes[:].bitcast(FP8X4), scales=scales[:], in_=qn_grouped[rnd][:]
             )

@@ -37,7 +37,7 @@ NORMALISE_LAG = 2
 TURN_QN_LAG = 3
 PRODUCT_2_LAG = 4
 FINISH_LAG = 5
-PREPARE_WQ_B_STEP = 2
+PREPARE_WQ_B_STEP = 1
 
 FLOPS = 2 * BATCH * SEQ * (DIM * Q_LORA + Q_LORA * HEADS * (NOPE + ROPE))
 
@@ -64,12 +64,6 @@ def tile_mla_pa_t_kernel(
         ps_nope = ctx.enter_context(tc.psum_pool(name="ps_nope", bufs=1))
         ps_rope = ctx.enter_context(tc.psum_pool(name="ps_rope", bufs=1))
 
-        def copy_out(index, out, in_):
-            if index % 2 == 0:
-                nc.scalar.copy(out=out, in_=in_)
-            else:
-                nc.vector.tensor_copy(out=out, in_=in_)
-
         x_rows = []
         for rnd in range(ROUNDS):
             x_round = keep.tile([P, ROUND_TILES, DIM], BF16, name="x_round%d" % rnd)
@@ -95,7 +89,6 @@ def tile_mla_pa_t_kernel(
         load_wq_a(2)
         load_wq_a(3)
         load_x(1)
-        load_x(2)
 
         wb_rows = keep.tile([P, HEADS + 1, Q_LORA], BF16)
         wb_heads = wq_b.rearrange("(h d) k -> d h k", h=HEADS)
@@ -105,7 +98,7 @@ def tile_mla_pa_t_kernel(
                 out=wb_rows[h * ROPE : (h + 1) * ROPE, HEADS, :],
                 in_=wb_heads[NOPE : NOPE + ROPE, h, :],
             )
-        for rnd in range(3, ROUNDS):
+        for rnd in range(2, ROUNDS):
             load_x(rnd)
 
         gain_row = keep.tile([P, Q_LORA], BF16)
@@ -202,37 +195,45 @@ def tile_mla_pa_t_kernel(
 
         wb_grouped = keep.tile([P, Q_COLS * PACK], BF16, align_bytes=256)
 
-        def prepare_wq_b():
-            grouped = wb_grouped
-            grouped_words = grouped[:].bitcast(F32).rearrange("p (n u) -> p n u", u=2)
+        def every_second_word(i):
+            words = wb_rows[:, i, :].bitcast(F32).rearrange("r (p u) -> r u p", u=2)
+            return [words[:, u, :] for u in range(2)]
 
-            def every_second_word(i):
-                words = wb_rows[:, i, :].bitcast(F32).rearrange("r (p u) -> r u p", u=2)
-                return [words[:, u, :] for u in range(2)]
+        wb_grouped_words = wb_grouped[:].bitcast(F32).rearrange("p (n u) -> p n u", u=2)
 
-            bank = idle_bank(1, 2 * HEADS)
-            turn_words(bank, every_second_word(0) + every_second_word(1))
-            nc.scalar.copy(
-                out=grouped_words[:, 0:NOPE_COLS, :].rearrange("p (i r) u -> p i r u", i=HEADS),
-                in_=bank[:].rearrange("p (i u) r -> p i r u", u=2),
-            )
+        def turn_rotated_rows():
             bank = idle_bank(2, 2)
             turn_words(bank, every_second_word(HEADS))
             nc.scalar.copy(
-                out=grouped_words[:, NOPE_COLS : NOPE_COLS + ROPE_COLS, :],
+                out=wb_grouped_words[:, NOPE_COLS : NOPE_COLS + ROPE_COLS, :],
                 in_=bank[:].rearrange("p u r -> p r u"),
             )
 
-        def exchange_wq_b():
+        def turn_copied_rows():
+            bank = idle_bank(1, 2 * HEADS)
+            turn_words(bank, every_second_word(0) + every_second_word(1))
+            nc.vector.tensor_copy(
+                out=wb_grouped_words[:, 0:NOPE_COLS, :].rearrange(
+                    "p (i r) u -> p i r u", i=HEADS
+                ),
+                in_=bank[:].rearrange("p (i u) r -> p i r u", u=2),
+            )
+
+        def exchange_rotated_rows():
             first = (NOPE_COLS + ROPE_COLS) * PACK
             row_pairs = wb_grouped[:, NOPE_COLS * PACK : first].rearrange(
                 "p (m e t) -> p m e t", e=2, t=PACK
             )
             swapped = wb_grouped[:, first:].rearrange("p (m e t) -> p m e t", e=2, t=PACK)
-            nc.vector.tensor_scalar_mul(
-                out=swapped[:, :, 0, :], in0=row_pairs[:, :, 1, :], scalar1=-1.0
-            )
-            nc.vector.tensor_copy(out=swapped[:, :, 1, :], in_=row_pairs[:, :, 0, :])
+            for e, sign in enumerate((-1.0, 1.0)):
+                nc.gpsimd.tensor_scalar(
+                    out=swapped[:, :, e, :],
+                    in0=row_pairs[:, :, 1 - e, :],
+                    scalar1=sign,
+                    scalar2=0.0,
+                    op0=ALU.mult,
+                    op1=ALU.add,
+                )
 
         def quantise_wq_b():
             nc.vector.quantize_mx(
@@ -251,23 +252,31 @@ def tile_mla_pa_t_kernel(
             turn_words(bank, blocks_of_row_words(x_rows[rnd][:, j, :].bitcast(F32)))
             x_banks[rnd].append(bank)
 
-        def copy_x(rnd, j):
+        def copy_x(rnd, j, copy):
             grouped_words = x_grouped[rnd][:].bitcast(F32).rearrange(
                 "p (j g r u) -> p j g r u", j=ROUND_TILES, g=PASSES_1, u=2
             )
-            copy_out(
-                j,
+            copy(
                 out=grouped_words[:, j],
                 in_=x_banks[rnd][j][:].rearrange("p (g u) r -> p g r u", u=2),
             )
 
-        def quantise_x(rnd):
-            codes = ring.tile([P, ROUND_TILES * PASSES_1 * P], U32, align_bytes=256, tag="x_codes")
-            scales = ring.tile([P, ROUND_TILES * PASSES_1 * P], U8, align_bytes=256, tag="x_scales")
+        def quantise_x(rnd, tiles=slice(0, ROUND_TILES)):
+            if tiles.start == 0:
+                codes = ring.tile(
+                    [P, ROUND_TILES * PASSES_1 * P], U32, align_bytes=256, tag="x_codes"
+                )
+                scales = ring.tile(
+                    [P, ROUND_TILES * PASSES_1 * P], U8, align_bytes=256, tag="x_scales"
+                )
+                x_mx[rnd] = (codes, scales)
+            codes, scales = x_mx[rnd]
+            toks = slice(tiles.start * PASSES_1 * P, tiles.stop * PASSES_1 * P)
             nc.vector.quantize_mx(
-                out=codes[:].bitcast(FP8X4), scales=scales[:], in_=x_grouped[rnd][:]
+                out=codes[:, toks].bitcast(FP8X4),
+                scales=scales[:, toks],
+                in_=x_grouped[rnd][:, toks.start * PACK : toks.stop * PACK],
             )
-            x_mx[rnd] = (codes, scales)
 
         def product_1(rnd):
             codes, scales = x_mx[rnd]
@@ -312,6 +321,7 @@ def tile_mla_pa_t_kernel(
         def normalise(rnd):
             rstd = rstd_of[rnd]
             qn = ring.tile([P, ROUND_TILES, Q_LORA], BF16, tag="qn")
+            qn_of[rnd] = qn
             for j in range(ROUND_TILES):
                 nc.vector.scalar_tensor_tensor(
                     out=qn[:, j, :],
@@ -321,7 +331,6 @@ def tile_mla_pa_t_kernel(
                     op0=ALU.mult,
                     op1=ALU.mult,
                 )
-            qn_of[rnd] = qn
 
         def turn_qn(rnd):
             qnt = ps_qnt.tile([P, ROUND_TILES * 2, P], F32, tag="qnt")
@@ -409,18 +418,19 @@ def tile_mla_pa_t_kernel(
                 stage_of_round(rnd)
 
         turn_x(0, 0)
-        copy_x(0, 0)
+        copy_x(0, 0, nc.vector.tensor_copy)
+        quantise_x(0, slice(0, 1))
         banks = turn_wq_a(0)
-        copy_wq_a(0, 0, banks[0], nc.vector.tensor_copy)
-        copy_wq_a(0, 1, banks[1], nc.scalar.copy)
+        copy_wq_a(0, 0, banks[0], nc.scalar.copy)
+        copy_wq_a(0, 1, banks[1], nc.vector.tensor_copy)
         turn_x(0, 1)
+        copy_x(0, 1, nc.scalar.copy)
         quantise_wq_a(0, 0)
         quantise_wq_a(0, 1)
-        copy_x(0, 1)
+        quantise_x(0, slice(1, 2))
         banks = turn_wq_a(1)
         copy_wq_a(1, 0, banks[0], nc.scalar.copy)
-        copy_wq_a(1, 1, banks[1], nc.scalar.copy)
-        quantise_x(0)
+        copy_wq_a(1, 1, banks[1], nc.vector.tensor_copy)
         quantise_wq_a(1, 0)
         quantise_wq_a(1, 1)
         spread_gain()
@@ -431,12 +441,10 @@ def tile_mla_pa_t_kernel(
             if step - FINISH_LAG in (-2, -1):
                 prepare_rotation(step - FINISH_LAG + 2)
             run(normalise, step - NORMALISE_LAG)
-            if step == PREPARE_WQ_B_STEP + 1:
-                exchange_wq_b()
             if step < ROUNDS:
                 for j in range(ROUND_TILES):
                     turn_x(step, j)
-                    copy_x(step, j)
+                    copy_x(step, j, (nc.scalar.copy, nc.vector.tensor_copy)[j])
             run(turn_qn, step - TURN_QN_LAG)
             run(copy_qn, step - TURN_QN_LAG)
             run(quantise_qn, step - TURN_QN_LAG)
@@ -444,10 +452,13 @@ def tile_mla_pa_t_kernel(
             if step == PREPARE_WQ_B_STEP + 1:
                 quantise_wq_b()
             run(product_1, step - PRODUCT_1_LAG)
-            run(root_mean_square, step - PRODUCT_1_LAG)
-            run(product_2, step - PRODUCT_2_LAG)
             if step == PREPARE_WQ_B_STEP:
-                prepare_wq_b()
+                turn_copied_rows()
+            run(root_mean_square, step - PRODUCT_1_LAG)
+            if step == PREPARE_WQ_B_STEP:
+                turn_rotated_rows()
+                exchange_rotated_rows()
+            run(product_2, step - PRODUCT_2_LAG)
 
         normalise(LAST)
         turn_qn(LAST - 1)

@@ -25,7 +25,7 @@ PASSES_1 = DIM // K_PASS
 WORD_BLOCKS = DIM // 2 // P
 NOPE_COLS = HEADS * NOPE
 ROPE_COLS = HEADS * ROPE
-Q_COLS = NOPE_COLS + 2 * ROPE_COLS
+Q_COLS = NOPE_COLS + ROPE_COLS
 
 ROUND_TILES = 2
 ROUNDS = BATCH * SEQ_TILES // ROUND_TILES
@@ -115,12 +115,15 @@ def tile_mla_pa_t_kernel(
         ones = keep.tile([P, P], BF16)
         nc.gpsimd.memset(ones[:], 1.0)
 
-        rot = keep.tile([P, SEQ_TILES, 2, ROPE], F32)
-
-        def prepare_rotation(c):
-            nc.scalar.copy(
-                out=rot[:, :, c, :].rearrange("p s (f e) -> p s f e", e=2),
-                in_=freqs_rows[:, c].unsqueeze(3).to_broadcast([P, SEQ_TILES, ROPE // 2, 2]),
+        signed_sin = keep.tile([P, SEQ_TILES, 2, ROPE // 2], F32)
+        for e, sign in enumerate((1.0, -1.0)):
+            nc.gpsimd.tensor_scalar(
+                out=signed_sin[:, :, e, :],
+                in0=freqs_rows[:, 1],
+                scalar1=sign,
+                scalar2=0.0,
+                op0=ALU.mult,
+                op1=ALU.add,
             )
 
         warm = keep.tile([P, 1], F32)
@@ -204,10 +207,16 @@ def tile_mla_pa_t_kernel(
         def turn_rotated_rows():
             bank = idle_bank(2, 2)
             turn_words(bank, every_second_word(HEADS))
-            nc.scalar.copy(
-                out=wb_grouped_words[:, NOPE_COLS : NOPE_COLS + ROPE_COLS, :],
-                in_=bank[:].rearrange("p u r -> p r u"),
-            )
+            for h in range(HEADS):
+                first = NOPE_COLS + h * ROPE
+                nc.scalar.copy(
+                    out=wb_grouped_words[:, first : first + ROPE, :].rearrange(
+                        "p (e f) u -> p e f u", e=2
+                    ),
+                    in_=bank[:, :, h * ROPE : (h + 1) * ROPE].rearrange(
+                        "p u (f e) -> p e f u", e=2
+                    ),
+                )
 
         def turn_copied_rows():
             bank = idle_bank(1, 2 * HEADS)
@@ -219,26 +228,13 @@ def tile_mla_pa_t_kernel(
                 in_=bank[:].rearrange("p (i u) r -> p i r u", u=2),
             )
 
-        def exchange_rotated_rows():
-            first = (NOPE_COLS + ROPE_COLS) * PACK
-            row_pairs = wb_grouped[:, NOPE_COLS * PACK : first].rearrange(
-                "p (m e t) -> p m e t", e=2, t=PACK
-            )
-            swapped = wb_grouped[:, first:].rearrange("p (m e t) -> p m e t", e=2, t=PACK)
-            for e, sign in enumerate((-1.0, 1.0)):
-                nc.gpsimd.tensor_scalar(
-                    out=swapped[:, :, e, :],
-                    in0=row_pairs[:, :, 1 - e, :],
-                    scalar1=sign,
-                    scalar2=0.0,
-                    op0=ALU.mult,
-                    op1=ALU.add,
-                )
-
         def quantise_wq_b():
-            nc.vector.quantize_mx(
-                out=wb_codes[:].bitcast(FP8X4), scales=wb_scales[:], in_=wb_grouped[:]
-            )
+            for cols in (slice(NOPE_COLS, Q_COLS), slice(0, NOPE_COLS)):
+                nc.vector.quantize_mx(
+                    out=wb_codes[:, cols].bitcast(FP8X4),
+                    scales=wb_scales[:, cols],
+                    in_=wb_grouped[:, cols.start * PACK : cols.stop * PACK],
+                )
 
         x_banks, x_grouped, x_mx, ql_banks, rstd_of = {}, {}, {}, {}, {}
         qn_of, qn_banks, qn_grouped, qn_mx, q_banks = {}, {}, {}, {}, {}
@@ -363,7 +359,7 @@ def tile_mla_pa_t_kernel(
             pool, tag = (ps_words, "words") if spare else (ps_nope, "nope_bank")
             nope_bank = pool.tile([P, ROUND_TILES, NOPE_COLS], F32, tag=tag, name="nope_bank")
             pool, tag = (ps_words, "words") if spare else (ps_rope, "rope_bank")
-            rope_bank = pool.tile([P, ROUND_TILES, 2 * ROPE_COLS], F32, tag=tag, name="rope_bank")
+            rope_bank = pool.tile([P, ROUND_TILES, ROPE_COLS], F32, tag=tag, name="rope_bank")
             for bank, cols in (
                 (rope_bank, slice(NOPE_COLS, Q_COLS)),
                 (nope_bank, slice(0, NOPE_COLS)),
@@ -393,22 +389,37 @@ def tile_mla_pa_t_kernel(
         def rotate(rnd):
             b, s0 = place(rnd)
             rope_bank = q_banks[rnd][1]
-            terms = once.tile([P, ROUND_TILES, 2 * ROPE_COLS], F32, tag="terms")
-            nc.vector.tensor_tensor(
-                out=terms[:].rearrange("p j (c h d) -> p (j c) h d", c=2, h=HEADS),
-                in0=rope_bank[:].rearrange("p j (c h d) -> p (j c) h d", c=2, h=HEADS),
-                in1=rot[:, s0 : s0 + ROUND_TILES]
-                .rearrange("p s c d -> p (s c) d")
+            if rnd > LAST - 3:
+                engine, v = nc.vector, rope_bank
+            else:
+                engine = nc.gpsimd
+                v = once.tile([P, ROUND_TILES, ROPE_COLS], F32, tag="v")
+                nc.vector.tensor_copy(out=v[:], in_=rope_bank[:])
+            toks = slice(s0, s0 + ROUND_TILES)
+            by_cos = ring.tile([P, ROUND_TILES, ROPE_COLS], F32, tag="by_cos")
+            engine.tensor_tensor(
+                out=by_cos[:].rearrange("p j (q f) -> p j q f", q=2 * HEADS),
+                in0=v[:].rearrange("p j (q f) -> p j q f", q=2 * HEADS),
+                in1=freqs_rows[:, 0, toks, :]
                 .unsqueeze(2)
-                .to_broadcast([P, 2 * ROUND_TILES, HEADS, ROPE]),
+                .to_broadcast([P, ROUND_TILES, 2 * HEADS, ROPE // 2]),
+                op=ALU.mult,
+            )
+            by_sin = ring.tile([P, ROUND_TILES, ROPE_COLS], F32, tag="by_sin")
+            engine.tensor_tensor(
+                out=by_sin[:].rearrange("p j (h d) -> p j h d", h=HEADS),
+                in0=v[:].rearrange("p j (h d) -> p j h d", h=HEADS),
+                in1=signed_sin[:, toks]
+                .rearrange("p s e f -> p s (e f)")
+                .unsqueeze(2)
+                .to_broadcast([P, ROUND_TILES, HEADS, ROPE]),
                 op=ALU.mult,
             )
             rope = once.tile([P, ROUND_TILES, ROPE_COLS], F32, tag="rope")
-            adder = nc.vector if rnd == LAST else nc.gpsimd
-            adder.tensor_tensor(
-                out=rope[:],
-                in0=terms[:, :, 0:ROPE_COLS],
-                in1=terms[:, :, ROPE_COLS : 2 * ROPE_COLS],
+            engine.tensor_tensor(
+                out=rope[:].rearrange("p j (h f e) -> p (j h) f e", h=HEADS, e=2),
+                in0=by_cos[:].rearrange("p j (h e f) -> p (j h) f e", h=HEADS, e=2),
+                in1=by_sin[:].rearrange("p j (h e f) -> p (j h) f e", h=HEADS, e=2)[:, :, :, ::-1],
                 op=ALU.add,
             )
             nc.sync.dma_start(out=rope_view[b, :, s0 : s0 + ROUND_TILES, :], in_=rope[:])
@@ -438,8 +449,6 @@ def tile_mla_pa_t_kernel(
         for step in range(1, ROUNDS + 1):
             run(copy_nope, step - FINISH_LAG)
             run(rotate, step - FINISH_LAG)
-            if step - FINISH_LAG in (-2, -1):
-                prepare_rotation(step - FINISH_LAG + 2)
             run(normalise, step - NORMALISE_LAG)
             if step < ROUNDS:
                 for j in range(ROUND_TILES):
@@ -457,7 +466,6 @@ def tile_mla_pa_t_kernel(
             run(root_mean_square, step - PRODUCT_1_LAG)
             if step == PREPARE_WQ_B_STEP:
                 turn_rotated_rows()
-                exchange_rotated_rows()
             run(product_2, step - PRODUCT_2_LAG)
 
         normalise(LAST)

@@ -237,6 +237,7 @@ def tile_mla_pa_t_kernel(
                 )
 
         x_banks, x_grouped, x_mx, ql_banks, rstd_of = {}, {}, {}, {}, {}
+        rope_values = {}
         qn_of, qn_banks, qn_grouped, qn_mx, q_banks = {}, {}, {}, {}, {}
 
         def turn_x(rnd, j):
@@ -274,10 +275,11 @@ def tile_mla_pa_t_kernel(
                 in_=x_grouped[rnd][:, toks.start * PACK : toks.stop * PACK],
             )
 
-        def product_1(rnd):
+        def product_1(rnd, tiles=range(ROUND_TILES)):
             codes, scales = x_mx[rnd]
-            ql_banks[rnd] = []
-            for j in range(ROUND_TILES):
+            if 0 in tiles:
+                ql_banks[rnd] = []
+            for j in tiles:
                 ql = ps_ql.tile([P, Q_LORA], F32, tag="ql")
                 for g in range(PASSES_1):
                     tok = slice((j * PASSES_1 + g) * P, (j * PASSES_1 + g + 1) * P)
@@ -292,11 +294,13 @@ def tile_mla_pa_t_kernel(
                     )
                 ql_banks[rnd].append(ql)
 
-        def root_mean_square(rnd):
-            sum_sq = once.tile([P, ROUND_TILES], F32, tag="sum_sq")
-            rstd = once.tile([P, ROUND_TILES], F32, tag="rstd")
-            root_tiles = 1 if rnd == LAST else ROUND_TILES
-            for j in range(ROUND_TILES):
+        def root_mean_square(rnd, tiles=range(ROUND_TILES)):
+            if 0 in tiles:
+                sum_sq = once.tile([P, ROUND_TILES], F32, tag="sum_sq")
+                rstd = once.tile([P, ROUND_TILES], F32, tag="rstd")
+                rstd_of[rnd] = (sum_sq, rstd)
+            sum_sq, rstd = rstd_of[rnd]
+            for j in tiles:
                 squares = pair.tile([P, Q_LORA], BF16, tag="squares")
                 nc.scalar.activation(
                     out=squares[:],
@@ -304,21 +308,25 @@ def tile_mla_pa_t_kernel(
                     func=ACT.Square,
                     accum_out=sum_sq[:, j : j + 1],
                 )
-                if (j + 1) % root_tiles == 0:
-                    nc.scalar.activation(
-                        out=rstd[:, j + 1 - root_tiles : j + 1],
-                        in_=sum_sq[:, j + 1 - root_tiles : j + 1],
-                        func=ACT.Abs_reciprocal_sqrt,
-                        bias=EPS,
-                        scale=1.0 / Q_LORA,
-                    )
-            rstd_of[rnd] = rstd
+                if rnd == LAST:
+                    root(rnd, slice(j, j + 1))
 
-        def normalise(rnd):
-            rstd = rstd_of[rnd]
-            qn = ring.tile([P, ROUND_TILES, Q_LORA], BF16, tag="qn")
-            qn_of[rnd] = qn
-            for j in range(ROUND_TILES):
+        def root(rnd, tiles=slice(0, ROUND_TILES)):
+            sum_sq, rstd = rstd_of[rnd]
+            nc.scalar.activation(
+                out=rstd[:, tiles],
+                in_=sum_sq[:, tiles],
+                func=ACT.Abs_reciprocal_sqrt,
+                bias=EPS,
+                scale=1.0 / Q_LORA,
+            )
+
+        def normalise(rnd, tiles=range(ROUND_TILES)):
+            rstd = rstd_of[rnd][1]
+            if 0 in tiles:
+                qn_of[rnd] = ring.tile([P, ROUND_TILES, Q_LORA], BF16, tag="qn", name="qn")
+            qn = qn_of[rnd]
+            for j in tiles:
                 nc.vector.scalar_tensor_tensor(
                     out=qn[:, j, :],
                     in0=ql_banks[rnd][j][:],
@@ -386,15 +394,19 @@ def tile_mla_pa_t_kernel(
             nc.scalar.copy(out=nope[:], in_=q_banks[rnd][0][:])
             nc.sync.dma_start(out=nope_view[b, :, s0 : s0 + ROUND_TILES, :], in_=nope[:])
 
+        def copy_rope(rnd, copy):
+            v = once.tile([P, ROUND_TILES, ROPE_COLS], F32, tag="v")
+            copy(out=v[:], in_=q_banks[rnd][1][:])
+            rope_values[rnd] = v
+
         def rotate(rnd):
             b, s0 = place(rnd)
             rope_bank = q_banks[rnd][1]
-            if rnd > LAST - 3:
+            if rnd not in rope_values:
                 engine, v = nc.vector, rope_bank
             else:
                 engine = nc.gpsimd
-                v = once.tile([P, ROUND_TILES, ROPE_COLS], F32, tag="v")
-                nc.vector.tensor_copy(out=v[:], in_=rope_bank[:])
+                v = rope_values[rnd]
             toks = slice(s0, s0 + ROUND_TILES)
             by_cos = ring.tile([P, ROUND_TILES, ROPE_COLS], F32, tag="by_cos")
             engine.tensor_tensor(
@@ -416,7 +428,8 @@ def tile_mla_pa_t_kernel(
                 op=ALU.mult,
             )
             rope = once.tile([P, ROUND_TILES, ROPE_COLS], F32, tag="rope")
-            engine.tensor_tensor(
+            adder = nc.vector if rnd >= LAST - 2 else nc.gpsimd
+            adder.tensor_tensor(
                 out=rope[:].rearrange("p j (h f e) -> p (j h) f e", h=HEADS, e=2),
                 in0=by_cos[:].rearrange("p j (h e f) -> p (j h) f e", h=HEADS, e=2),
                 in1=by_sin[:].rearrange("p j (h e f) -> p (j h) f e", h=HEADS, e=2)[:, :, :, ::-1],
@@ -446,39 +459,44 @@ def tile_mla_pa_t_kernel(
         quantise_wq_a(1, 1)
         spread_gain()
 
+        S, V = nc.scalar.copy, nc.vector.tensor_copy
         for step in range(1, ROUNDS + 1):
-            run(copy_nope, step - FINISH_LAG)
-            run(rotate, step - FINISH_LAG)
-            run(normalise, step - NORMALISE_LAG)
-            if step < ROUNDS:
-                for j in range(ROUND_TILES):
-                    turn_x(step, j)
-                    copy_x(step, j, (nc.scalar.copy, nc.vector.tensor_copy)[j])
-            run(turn_qn, step - TURN_QN_LAG)
-            run(copy_qn, step - TURN_QN_LAG)
-            run(quantise_qn, step - TURN_QN_LAG)
-            run(quantise_x, step)
-            if step == PREPARE_WQ_B_STEP + 1:
+            n = step
+            run(lambda r: root(r, slice(0, 1)), n - 2)
+            if n < ROUNDS:
+                turn_x(n, 0)
+                copy_x(n, 0, S)
+                turn_x(n, 1)
+            run(lambda r: root(r, slice(1, 2)), n - 2)
+            run(lambda r: normalise(r, [0]), n - 2)
+            if n < ROUNDS:
+                copy_x(n, 1, V)
+            run(turn_qn, n - 3)
+            run(copy_qn, n - 3)
+            run(product_2, n - 4)
+            run(lambda r: normalise(r, [1]), n - 2)
+            run(lambda r: copy_rope(r, V) if r <= LAST - 4 else None, n - 4)
+            run(copy_nope, n - 4)
+            run(quantise_qn, n - 3)
+            run(quantise_x, n)
+            if n == PREPARE_WQ_B_STEP + 1:
                 quantise_wq_b()
-            run(product_1, step - PRODUCT_1_LAG)
-            if step == PREPARE_WQ_B_STEP:
+            run(rotate, n - 4)
+            run(product_1, n - 1)
+            if n == PREPARE_WQ_B_STEP:
                 turn_copied_rows()
-            run(root_mean_square, step - PRODUCT_1_LAG)
-            if step == PREPARE_WQ_B_STEP:
+            run(root_mean_square, n - 1)
+            if n == PREPARE_WQ_B_STEP:
                 turn_rotated_rows()
-            run(product_2, step - PRODUCT_2_LAG)
-
         normalise(LAST)
         turn_qn(LAST - 1)
         copy_qn(LAST - 1)
-        copy_nope(LAST - 3)
-        rotate(LAST - 3)
         quantise_qn(LAST - 1)
         product_2(LAST - 2)
-        turn_qn(LAST)
-        copy_qn(LAST)
         copy_nope(LAST - 2)
         rotate(LAST - 2)
+        turn_qn(LAST)
+        copy_qn(LAST)
         quantise_qn(LAST)
         product_2(LAST - 1)
         copy_nope(LAST - 1)

@@ -115,16 +115,18 @@ def tile_mla_pa_t_kernel(
         ones = keep.tile([P, P], BF16)
         nc.gpsimd.memset(ones[:], 1.0)
 
-        signed_sin = keep.tile([P, SEQ_TILES, 2, ROPE // 2], F32)
+        rot_cos = keep.tile([P, SEQ_TILES, ROPE // 2, 2], F32)
+        rot_sin = keep.tile([P, SEQ_TILES, ROPE // 2, 2], F32)
         for e, sign in enumerate((1.0, -1.0)):
-            nc.gpsimd.tensor_scalar(
-                out=signed_sin[:, :, e, :],
-                in0=freqs_rows[:, 1],
-                scalar1=sign,
-                scalar2=0.0,
-                op0=ALU.mult,
-                op1=ALU.add,
-            )
+            for table, freqs, factor in ((rot_cos, 0, 1.0), (rot_sin, 1, sign)):
+                nc.gpsimd.tensor_scalar(
+                    out=table[:, :, :, e],
+                    in0=freqs_rows[:, freqs],
+                    scalar1=factor,
+                    scalar2=0.0,
+                    op0=ALU.mult,
+                    op1=ALU.add,
+                )
 
         warm = keep.tile([P, 1], F32)
         nc.scalar.activation(out=warm[:], in_=ones[:, 0:1], func=ACT.Abs_reciprocal_sqrt)
@@ -207,20 +209,17 @@ def tile_mla_pa_t_kernel(
         def turn_rotated_rows():
             bank = idle_bank(2, 2)
             turn_words(bank, every_second_word(HEADS))
-            for h in range(HEADS):
-                first = NOPE_COLS + h * ROPE
-                nc.scalar.copy(
-                    out=wb_grouped_words[:, first : first + ROPE, :].rearrange(
-                        "p (e f) u -> p e f u", e=2
-                    ),
-                    in_=bank[:, :, h * ROPE : (h + 1) * ROPE].rearrange(
-                        "p u (f e) -> p e f u", e=2
-                    ),
-                )
+            nc.scalar.copy(
+                out=wb_grouped_words[:, NOPE_COLS : NOPE_COLS + ROPE_COLS, :],
+                in_=bank[:].rearrange("p u r -> p r u"),
+            )
 
         def turn_copied_rows():
             bank = idle_bank(1, 2 * HEADS)
             turn_words(bank, every_second_word(0) + every_second_word(1))
+            return bank
+
+        def copy_copied_rows(bank):
             nc.vector.tensor_copy(
                 out=wb_grouped_words[:, 0:NOPE_COLS, :].rearrange(
                     "p (i r) u -> p i r u", i=HEADS
@@ -228,8 +227,8 @@ def tile_mla_pa_t_kernel(
                 in_=bank[:].rearrange("p (i u) r -> p i r u", u=2),
             )
 
-        def quantise_wq_b():
-            for cols in (slice(NOPE_COLS, Q_COLS), slice(0, NOPE_COLS)):
+        def quantise_wq_b(parts):
+            for cols in parts:
                 nc.vector.quantize_mx(
                     out=wb_codes[:, cols].bitcast(FP8X4),
                     scales=wb_scales[:, cols],
@@ -363,10 +362,10 @@ def tile_mla_pa_t_kernel(
 
         def product_2(rnd):
             codes, scales = qn_mx[rnd]
-            spare = rnd in (LAST - 2, LAST)
-            pool, tag = (ps_words, "words") if spare else (ps_nope, "nope_bank")
+            spare = {LAST - 2: (ps_words, "words"), LAST: (ps_ql, "ql")}
+            pool, tag = spare.get(rnd, (ps_nope, "nope_bank"))
             nope_bank = pool.tile([P, ROUND_TILES, NOPE_COLS], F32, tag=tag, name="nope_bank")
-            pool, tag = (ps_words, "words") if spare else (ps_rope, "rope_bank")
+            pool, tag = spare.get(rnd, (ps_rope, "rope_bank"))
             rope_bank = pool.tile([P, ROUND_TILES, ROPE_COLS], F32, tag=tag, name="rope_bank")
             for bank, cols in (
                 (rope_bank, slice(NOPE_COLS, Q_COLS)),
@@ -407,32 +406,24 @@ def tile_mla_pa_t_kernel(
             else:
                 engine = nc.gpsimd
                 v = rope_values[rnd]
-            toks = slice(s0, s0 + ROUND_TILES)
             by_cos = ring.tile([P, ROUND_TILES, ROPE_COLS], F32, tag="by_cos")
-            engine.tensor_tensor(
-                out=by_cos[:].rearrange("p j (q f) -> p j q f", q=2 * HEADS),
-                in0=v[:].rearrange("p j (q f) -> p j q f", q=2 * HEADS),
-                in1=freqs_rows[:, 0, toks, :]
-                .unsqueeze(2)
-                .to_broadcast([P, ROUND_TILES, 2 * HEADS, ROPE // 2]),
-                op=ALU.mult,
-            )
             by_sin = ring.tile([P, ROUND_TILES, ROPE_COLS], F32, tag="by_sin")
-            engine.tensor_tensor(
-                out=by_sin[:].rearrange("p j (h d) -> p j h d", h=HEADS),
-                in0=v[:].rearrange("p j (h d) -> p j h d", h=HEADS),
-                in1=signed_sin[:, toks]
-                .rearrange("p s e f -> p s (e f)")
-                .unsqueeze(2)
-                .to_broadcast([P, ROUND_TILES, HEADS, ROPE]),
-                op=ALU.mult,
-            )
+            for product, table in ((by_cos, rot_cos), (by_sin, rot_sin)):
+                engine.tensor_tensor(
+                    out=product[:].rearrange("p j (h d) -> p j h d", h=HEADS),
+                    in0=v[:].rearrange("p j (h d) -> p j h d", h=HEADS),
+                    in1=table[:, s0 : s0 + ROUND_TILES]
+                    .rearrange("p s f e -> p s (f e)")
+                    .unsqueeze(2)
+                    .to_broadcast([P, ROUND_TILES, HEADS, ROPE]),
+                    op=ALU.mult,
+                )
             rope = once.tile([P, ROUND_TILES, ROPE_COLS], F32, tag="rope")
             adder = nc.vector if rnd >= LAST - 2 else nc.gpsimd
             adder.tensor_tensor(
-                out=rope[:].rearrange("p j (h f e) -> p (j h) f e", h=HEADS, e=2),
-                in0=by_cos[:].rearrange("p j (h e f) -> p (j h) f e", h=HEADS, e=2),
-                in1=by_sin[:].rearrange("p j (h e f) -> p (j h) f e", h=HEADS, e=2)[:, :, :, ::-1],
+                out=rope[:].rearrange("p j (m e) -> p (j m) e", e=2),
+                in0=by_cos[:].rearrange("p j (m e) -> p (j m) e", e=2),
+                in1=by_sin[:].rearrange("p j (m e) -> p (j m) e", e=2)[:, :, ::-1],
                 op=ALU.add,
             )
             nc.sync.dma_start(out=rope_view[b, :, s0 : s0 + ROUND_TILES, :], in_=rope[:])
@@ -479,14 +470,18 @@ def tile_mla_pa_t_kernel(
             run(copy_nope, n - 4)
             run(quantise_qn, n - 3)
             run(quantise_x, n)
-            if n == PREPARE_WQ_B_STEP + 1:
-                quantise_wq_b()
+            if n == 2:
+                quantise_wq_b([slice(0, NOPE_COLS)])
+            if n == 3:
+                quantise_wq_b([slice(NOPE_COLS, Q_COLS)])
             run(rotate, n - 4)
             run(product_1, n - 1)
-            if n == PREPARE_WQ_B_STEP:
-                turn_copied_rows()
+            if n == 1:
+                wb_bank = turn_copied_rows()
             run(root_mean_square, n - 1)
-            if n == PREPARE_WQ_B_STEP:
+            if n == 1:
+                copy_copied_rows(wb_bank)
+            if n == 2:
                 turn_rotated_rows()
         normalise(LAST)
         turn_qn(LAST - 1)

@@ -31,6 +31,7 @@ ROUND_TILES = 2
 ROUNDS = BATCH * SEQ_TILES // ROUND_TILES
 ROUNDS_PER_BATCH = SEQ_TILES // ROUND_TILES
 LAST = ROUNDS - 1
+FREQS_AFTER = 2
 
 PRODUCT_1_LAG = 1
 NORMALISE_LAG = 2
@@ -98,35 +99,35 @@ def tile_mla_pa_t_kernel(
                 out=wb_rows[h * ROPE : (h + 1) * ROPE, HEADS, :],
                 in_=wb_heads[NOPE : NOPE + ROPE, h, :],
             )
+        freqs_rows = keep.tile([P, 2, SEQ_TILES, ROPE // 2], BF16)
         for rnd in range(2, ROUNDS):
             load_x(rnd)
+            if rnd == FREQS_AFTER:
+                for c, freqs in enumerate((freqs_cos, freqs_sin)):
+                    nc.sync.dma_start(
+                        out=freqs_rows[:, c], in_=freqs.rearrange("(p s) f -> p s f", s=SEQ_TILES)
+                    )
 
         gain_row = keep.tile([P, Q_LORA], BF16)
         nc.gpsimd.memset(gain_row[:], 0.0)
         nc.scalar.dma_start(out=gain_row[0:1, :], in_=q_norm_w.rearrange("(o n) -> o n", o=1))
-        freqs_rows = keep.tile([P, 2, SEQ_TILES, ROPE // 2], BF16)
-        for c, freqs in enumerate((freqs_cos, freqs_sin)):
-            nc.scalar.dma_start(
-                out=freqs_rows[:, c], in_=freqs.rearrange("(p s) f -> p s f", s=SEQ_TILES)
-            )
 
         ident_f32 = keep.tile([P, P], F32)
         make_identity(nc, ident_f32[:])
         ones = keep.tile([P, P], BF16)
         nc.gpsimd.memset(ones[:], 1.0)
 
-        rot_cos = keep.tile([P, SEQ_TILES, ROPE // 2, 2], F32)
-        rot_sin = keep.tile([P, SEQ_TILES, ROPE // 2, 2], F32)
-        for e, sign in enumerate((1.0, -1.0)):
-            for table, freqs, factor in ((rot_cos, 0, 1.0), (rot_sin, 1, sign)):
-                nc.gpsimd.tensor_scalar(
-                    out=table[:, :, :, e],
-                    in0=freqs_rows[:, freqs],
-                    scalar1=factor,
-                    scalar2=0.0,
-                    op0=ALU.mult,
-                    op1=ALU.add,
-                )
+        rot = keep.tile([P, 2, SEQ_TILES, 2 * HEADS, ROPE // 2], F32)
+
+        def prepare_rotation(c):
+            nc.gpsimd.tensor_scalar(
+                out=rot[:, c],
+                in0=freqs_rows[:, c].unsqueeze(2).to_broadcast([P, SEQ_TILES, 2 * HEADS, ROPE // 2]),
+                scalar1=1.0,
+                scalar2=0.0,
+                op0=ALU.mult,
+                op1=ALU.add,
+            )
 
         warm = keep.tile([P, 1], F32)
         nc.scalar.activation(out=warm[:], in_=ones[:, 0:1], func=ACT.Abs_reciprocal_sqrt)
@@ -210,8 +211,10 @@ def tile_mla_pa_t_kernel(
             bank = idle_bank(2, 2)
             turn_words(bank, every_second_word(HEADS))
             nc.scalar.copy(
-                out=wb_grouped_words[:, NOPE_COLS : NOPE_COLS + ROPE_COLS, :],
-                in_=bank[:].rearrange("p u r -> p r u"),
+                out=wb_grouped_words[:, NOPE_COLS : NOPE_COLS + ROPE_COLS, :].rearrange(
+                    "p (e m) u -> p e m u", e=2
+                ),
+                in_=bank[:].rearrange("p u (m e) -> p e m u", e=2),
             )
 
         def turn_copied_rows():
@@ -402,30 +405,31 @@ def tile_mla_pa_t_kernel(
             b, s0 = place(rnd)
             rope_bank = q_banks[rnd][1]
             if rnd not in rope_values:
-                engine, v = nc.vector, rope_bank
+                engine, v = nc.vector, rope_bank[:]
             else:
                 engine = nc.gpsimd
-                v = rope_values[rnd]
-            by_cos = ring.tile([P, ROUND_TILES, ROPE_COLS], F32, tag="by_cos")
-            by_sin = ring.tile([P, ROUND_TILES, ROPE_COLS], F32, tag="by_sin")
-            for product, table in ((by_cos, rot_cos), (by_sin, rot_sin)):
+                v = rope_values[rnd][:]
+            products = []
+            for c in range(2):
+                product = ring.tile([P, ROUND_TILES, ROPE_COLS], F32, tag="product%d" % c, name="product")
                 engine.tensor_tensor(
-                    out=product[:].rearrange("p j (h d) -> p j h d", h=HEADS),
-                    in0=v[:].rearrange("p j (h d) -> p j h d", h=HEADS),
-                    in1=table[:, s0 : s0 + ROUND_TILES]
-                    .rearrange("p s f e -> p s (f e)")
-                    .unsqueeze(2)
-                    .to_broadcast([P, ROUND_TILES, HEADS, ROPE]),
+                    out=product[:],
+                    in0=v,
+                    in1=rot[:, c, s0 : s0 + ROUND_TILES].rearrange("p s q f -> p s (q f)"),
                     op=ALU.mult,
                 )
+                products.append(product[:].rearrange("p j (e m) -> p j e m", e=2))
+            by_cos, by_sin = products
             rope = once.tile([P, ROUND_TILES, ROPE_COLS], F32, tag="rope")
-            adder = nc.vector if rnd >= LAST - 2 else nc.gpsimd
-            adder.tensor_tensor(
-                out=rope[:].rearrange("p j (m e) -> p (j m) e", e=2),
-                in0=by_cos[:].rearrange("p j (m e) -> p (j m) e", e=2),
-                in1=by_sin[:].rearrange("p j (m e) -> p (j m) e", e=2)[:, :, ::-1],
-                op=ALU.add,
-            )
+            rope_pairs = rope[:].rearrange("p j (m e) -> p j m e", e=2)
+            adder = nc.vector if rnd == LAST else nc.gpsimd
+            for e, op in enumerate((ALU.subtract, ALU.add)):
+                adder.tensor_tensor(
+                    out=rope_pairs[:, :, :, e],
+                    in0=by_cos[:, :, e, :],
+                    in1=by_sin[:, :, 1 - e, :],
+                    op=op,
+                )
             nc.sync.dma_start(out=rope_view[b, :, s0 : s0 + ROUND_TILES, :], in_=rope[:])
 
         def run(stage_of_round, rnd):
@@ -451,6 +455,8 @@ def tile_mla_pa_t_kernel(
         spread_gain()
 
         S, V = nc.scalar.copy, nc.vector.tensor_copy
+        prepare_rotation(0)
+        prepare_rotation(1)
         for step in range(1, ROUNDS + 1):
             n = step
             run(lambda r: root(r, slice(0, 1)), n - 2)

@@ -32,6 +32,7 @@ ROUNDS = BATCH * SEQ_TILES // ROUND_TILES
 ROUNDS_PER_BATCH = SEQ_TILES // ROUND_TILES
 LAST = ROUNDS - 1
 FREQS_AFTER = 2
+GPSIMD_COLS = 192
 
 PRODUCT_1_LAG = 1
 NORMALISE_LAG = 2
@@ -117,13 +118,13 @@ def tile_mla_pa_t_kernel(
         ones = keep.tile([P, P], BF16)
         nc.gpsimd.memset(ones[:], 1.0)
 
-        rot = keep.tile([P, 2, SEQ_TILES, 2 * HEADS, ROPE // 2], F32)
+        rot = keep.tile([P, 2, SEQ_TILES, 2, HEADS * ROPE // 2], F32)
 
-        def prepare_rotation(c):
+        def prepare_rotation(c, e, sign):
             nc.gpsimd.tensor_scalar(
-                out=rot[:, c],
-                in0=freqs_rows[:, c].unsqueeze(2).to_broadcast([P, SEQ_TILES, 2 * HEADS, ROPE // 2]),
-                scalar1=1.0,
+                out=rot[:, c, :, e].rearrange("p s (h f) -> p s h f", h=HEADS),
+                in0=freqs_rows[:, c].unsqueeze(2).to_broadcast([P, SEQ_TILES, HEADS, ROPE // 2]),
+                scalar1=sign,
                 scalar2=0.0,
                 op0=ALU.mult,
                 op1=ALU.add,
@@ -239,7 +240,7 @@ def tile_mla_pa_t_kernel(
                 )
 
         x_banks, x_grouped, x_mx, ql_banks, rstd_of = {}, {}, {}, {}, {}
-        rope_values = {}
+        rope_values, products_of = {}, {}
         qn_of, qn_banks, qn_grouped, qn_mx, q_banks = {}, {}, {}, {}, {}
 
         def turn_x(rnd, j):
@@ -396,40 +397,43 @@ def tile_mla_pa_t_kernel(
             nc.scalar.copy(out=nope[:], in_=q_banks[rnd][0][:])
             nc.sync.dma_start(out=nope_view[b, :, s0 : s0 + ROUND_TILES, :], in_=nope[:])
 
+        def multiply(rnd, engine, values, cols):
+            s0 = place(rnd)[1]
+            factors = rot[:, :, s0 : s0 + ROUND_TILES].rearrange("p c s e q -> p c (s e q)")
+            n = cols.stop - cols.start
+            engine.tensor_tensor(
+                out=products_of[rnd][:, :, cols],
+                in0=values.unsqueeze(1).to_broadcast([P, 2, n]),
+                in1=factors[:, :, cols],
+                op=ALU.mult,
+            )
+
         def copy_rope(rnd, copy):
-            v = once.tile([P, ROUND_TILES, ROPE_COLS], F32, tag="v")
-            copy(out=v[:], in_=q_banks[rnd][1][:])
-            rope_values[rnd] = v
+            rope_bank = q_banks[rnd][1][:].rearrange("p j q -> p (j q)")
+            products_of[rnd] = ring.tile([P, 2, ROUND_TILES * ROPE_COLS], F32, tag="products", name="products")
+            g_cols = GPSIMD_COLS if copy is not None else 0
+            if g_cols < ROUND_TILES * ROPE_COLS:
+                cols = slice(g_cols, ROUND_TILES * ROPE_COLS)
+                multiply(rnd, nc.vector, rope_bank[:, cols], cols)
+            if g_cols:
+                v = once.tile([P, GPSIMD_COLS], F32, tag="v")
+                copy(out=v[:], in_=rope_bank[:, 0:GPSIMD_COLS])
+                rope_values[rnd] = v
 
         def rotate(rnd):
             b, s0 = place(rnd)
-            rope_bank = q_banks[rnd][1]
-            if rnd not in rope_values:
-                engine, v = nc.vector, rope_bank[:]
-            else:
-                engine = nc.gpsimd
-                v = rope_values[rnd][:]
-            products = []
-            for c in range(2):
-                product = ring.tile([P, ROUND_TILES, ROPE_COLS], F32, tag="product%d" % c, name="product")
-                engine.tensor_tensor(
-                    out=product[:],
-                    in0=v,
-                    in1=rot[:, c, s0 : s0 + ROUND_TILES].rearrange("p s q f -> p s (q f)"),
-                    op=ALU.mult,
-                )
-                products.append(product[:].rearrange("p j (e m) -> p j e m", e=2))
-            by_cos, by_sin = products
+            if rnd in rope_values:
+                multiply(rnd, nc.gpsimd, rope_values[rnd][:], slice(0, GPSIMD_COLS))
+            products = products_of[rnd]
             rope = once.tile([P, ROUND_TILES, ROPE_COLS], F32, tag="rope")
-            rope_pairs = rope[:].rearrange("p j (m e) -> p j m e", e=2)
             adder = nc.vector if rnd == LAST else nc.gpsimd
-            for e, op in enumerate((ALU.subtract, ALU.add)):
-                adder.tensor_tensor(
-                    out=rope_pairs[:, :, :, e],
-                    in0=by_cos[:, :, e, :],
-                    in1=by_sin[:, :, 1 - e, :],
-                    op=op,
-                )
+            by_value = products[:].rearrange("p c (j e m) -> p c j e m", e=2, j=ROUND_TILES)
+            adder.tensor_tensor(
+                out=rope[:].rearrange("p j (m e) -> p j e m", e=2),
+                in0=by_value[:, 0],
+                in1=by_value[:, 1, :, ::-1, :],
+                op=ALU.add,
+            )
             nc.sync.dma_start(out=rope_view[b, :, s0 : s0 + ROUND_TILES, :], in_=rope[:])
 
         def run(stage_of_round, rnd):
@@ -455,8 +459,9 @@ def tile_mla_pa_t_kernel(
         spread_gain()
 
         S, V = nc.scalar.copy, nc.vector.tensor_copy
-        prepare_rotation(0)
-        prepare_rotation(1)
+        for e, sign in enumerate((1.0, -1.0)):
+            prepare_rotation(0, e, 1.0)
+            prepare_rotation(1, e, sign)
         for step in range(1, ROUNDS + 1):
             n = step
             run(lambda r: root(r, slice(0, 1)), n - 2)
@@ -472,7 +477,7 @@ def tile_mla_pa_t_kernel(
             run(copy_qn, n - 3)
             run(product_2, n - 4)
             run(lambda r: normalise(r, [1]), n - 2)
-            run(lambda r: copy_rope(r, V) if r <= LAST - 4 else None, n - 4)
+            run(lambda r: copy_rope(r, V if r <= LAST - 4 else None), n - 4)
             run(copy_nope, n - 4)
             run(quantise_qn, n - 3)
             run(quantise_x, n)
@@ -495,13 +500,16 @@ def tile_mla_pa_t_kernel(
         quantise_qn(LAST - 1)
         product_2(LAST - 2)
         copy_nope(LAST - 2)
+        copy_rope(LAST - 2, None)
         rotate(LAST - 2)
         turn_qn(LAST)
         copy_qn(LAST)
         quantise_qn(LAST)
         product_2(LAST - 1)
         copy_nope(LAST - 1)
+        copy_rope(LAST - 1, None)
         rotate(LAST - 1)
         product_2(LAST)
         copy_nope(LAST)
+        copy_rope(LAST, None)
         rotate(LAST)

@@ -60,6 +60,7 @@ def tile_mla_pa_t_kernel(
         pair = ctx.enter_context(tc.tile_pool(name="pair", bufs=2))
         ring = ctx.enter_context(tc.tile_pool(name="ring", bufs=3))
         once = ctx.enter_context(tc.tile_pool(name="once", bufs=ROUNDS))
+        early = ctx.enter_context(tc.tile_pool(name="early", bufs=LAST - 3))
         ps_words = ctx.enter_context(tc.psum_pool(name="ps_words", bufs=2))
         ps_ql = ctx.enter_context(tc.psum_pool(name="ps_ql", bufs=3))
         ps_qnt = ctx.enter_context(tc.psum_pool(name="ps_qnt", bufs=1))
@@ -339,6 +340,83 @@ def tile_mla_pa_t_kernel(
                     op1=ALU.mult,
                 )
 
+        def turn_qn_tile(rnd, j):
+            pool, tag = ((ps_ql, "ql"), (ps_qnt, "qnt"))[j]
+            qnt = pool.tile([P, 2, P], F32, tag=tag, name="qnt")
+            words = qn_of[rnd][:, j, :].bitcast(F32)
+            turn_words(qnt, [words[:, v * P : (v + 1) * P] for v in range(2)])
+            qn_banks[rnd, j] = qnt
+
+        def copy_qn_tile(rnd, j, copy):
+            if j == 0:
+                qn_grouped[rnd] = pair.tile([P, ROUND_TILES * Q_LORA], BF16, align_bytes=256, tag="qn_grouped", name="grouped")
+            copy(
+                out=qn_grouped[rnd][:, j * Q_LORA : (j + 1) * Q_LORA].bitcast(F32).rearrange("p (r v) -> p r v", v=2),
+                in_=qn_banks[rnd, j][:].rearrange("p v r -> p r v"),
+            )
+
+        def quantise_qn_tile(rnd, j):
+            if j == 0:
+                codes = ring.tile([P, ROUND_TILES * P], U32, align_bytes=256, tag="qn_codes")
+                scales = ring.tile([P, ROUND_TILES * P], U8, align_bytes=256, tag="qn_scales")
+                qn_mx[rnd] = (codes, scales)
+            codes, scales = qn_mx[rnd]
+            toks = slice(j * P, (j + 1) * P)
+            nc.vector.quantize_mx(
+                out=codes[:, toks].bitcast(FP8X4), scales=scales[:, toks],
+                in_=qn_grouped[rnd][:, j * Q_LORA : (j + 1) * Q_LORA],
+            )
+
+        def product_2_tile(rnd, j):
+            codes, scales = qn_mx[rnd]
+            rope_bank = ps_ql.tile([P, ROPE_COLS], F32, tag="ql", name="rope_bank")
+            pool, tag = ((ps_ql, "ql"), (ps_words, "words"))[j]
+            nope_bank = pool.tile([P, NOPE_COLS], F32, tag=tag, name="nope_bank")
+            tok = slice(j * P, (j + 1) * P)
+            for bank, cols in (
+                (rope_bank, slice(NOPE_COLS, Q_COLS)),
+                (nope_bank, slice(0, NOPE_COLS)),
+            ):
+                nc.tensor.matmul_mx(
+                    out=bank[:],
+                    lhsT=codes[:, tok].bitcast(FP8X4),
+                    lhsT_scale=scales[:, tok],
+                    rhs=wb_codes[:, cols].bitcast(FP8X4),
+                    rhs_scale=wb_scales[:, cols],
+                    start=True,
+                    stop=True,
+                )
+            q_banks[rnd, j] = (nope_bank, rope_bank)
+
+        def copy_nope_of_tile(rnd, j):
+            b, s0 = place(rnd)
+            nope = once.tile([P, NOPE_COLS], F32, tag="nope_tile%d" % j, name="nope_tile", bufs=1)
+            nc.scalar.copy(out=nope[:], in_=q_banks[rnd, j][0][:])
+            nc.sync.dma_start(out=nope_view[b, :, s0 + j, :], in_=nope[:])
+
+        def multiply_tile(rnd, j):
+            s0 = place(rnd)[1]
+            products = once.tile([P, 2, ROPE_COLS], F32, tag="products_tile%d" % j, name="products_tile", bufs=1)
+            nc.vector.tensor_tensor(
+                out=products[:],
+                in0=q_banks[rnd, j][1][:].unsqueeze(1).to_broadcast([P, 2, ROPE_COLS]),
+                in1=rot[:, :, s0 + j].rearrange("p c e q -> p c (e q)"),
+                op=ALU.mult,
+            )
+            products_of[rnd, j] = products
+
+        def sum_tile(rnd, j):
+            b, s0 = place(rnd)
+            rope = once.tile([P, ROPE_COLS], F32, tag="rope_tile%d" % j, name="rope_tile", bufs=1)
+            by_value = products_of[rnd, j][:].rearrange("p c (e m) -> p c e m", e=2)
+            nc.vector.tensor_tensor(
+                out=rope[:].rearrange("p (m e) -> p e m", e=2),
+                in0=by_value[:, 0],
+                in1=by_value[:, 1, ::-1, :],
+                op=ALU.add,
+            )
+            nc.sync.dma_start(out=rope_view[b, :, s0 + j, :], in_=rope[:])
+
         def turn_qn(rnd):
             qnt = ps_qnt.tile([P, ROUND_TILES * 2, P], F32, tag="qnt")
             blocks = []
@@ -357,8 +435,8 @@ def tile_mla_pa_t_kernel(
             qn_grouped[rnd] = grouped
 
         def quantise_qn(rnd):
-            codes = once.tile([P, ROUND_TILES * P], U32, align_bytes=256, tag="qn_codes")
-            scales = once.tile([P, ROUND_TILES * P], U8, align_bytes=256, tag="qn_scales")
+            codes = ring.tile([P, ROUND_TILES * P], U32, align_bytes=256, tag="qn_codes")
+            scales = ring.tile([P, ROUND_TILES * P], U8, align_bytes=256, tag="qn_scales")
             nc.vector.quantize_mx(
                 out=codes[:].bitcast(FP8X4), scales=scales[:], in_=qn_grouped[rnd][:]
             )
@@ -410,13 +488,14 @@ def tile_mla_pa_t_kernel(
 
         def copy_rope(rnd, copy):
             rope_bank = q_banks[rnd][1][:].rearrange("p j q -> p (j q)")
-            products_of[rnd] = ring.tile([P, 2, ROUND_TILES * ROPE_COLS], F32, tag="products", name="products")
             g_cols = GPSIMD_COLS if copy is not None else 0
+            pool, tag = (early, "products") if g_cols else (ring, "last_products")
+            products_of[rnd] = pool.tile([P, 2, ROUND_TILES * ROPE_COLS], F32, tag=tag, name="products")
             if g_cols < ROUND_TILES * ROPE_COLS:
                 cols = slice(g_cols, ROUND_TILES * ROPE_COLS)
                 multiply(rnd, nc.vector, rope_bank[:, cols], cols)
             if g_cols:
-                v = once.tile([P, GPSIMD_COLS], F32, tag="v")
+                v = early.tile([P, GPSIMD_COLS], F32, tag="v")
                 copy(out=v[:], in_=rope_bank[:, 0:GPSIMD_COLS])
                 rope_values[rnd] = v
 
@@ -426,7 +505,7 @@ def tile_mla_pa_t_kernel(
                 multiply(rnd, nc.gpsimd, rope_values[rnd][:], slice(0, GPSIMD_COLS))
             products = products_of[rnd]
             rope = once.tile([P, ROUND_TILES, ROPE_COLS], F32, tag="rope")
-            adder = nc.vector if rnd == LAST else nc.gpsimd
+            adder = nc.vector if rnd >= LAST - 2 else nc.gpsimd
             by_value = products[:].rearrange("p c (j e m) -> p c j e m", e=2, j=ROUND_TILES)
             adder.tensor_tensor(
                 out=rope[:].rearrange("p j (m e) -> p j e m", e=2),
@@ -494,22 +573,30 @@ def tile_mla_pa_t_kernel(
                 copy_copied_rows(wb_bank)
             if n == 2:
                 turn_rotated_rows()
-        normalise(LAST)
         turn_qn(LAST - 1)
         copy_qn(LAST - 1)
-        quantise_qn(LAST - 1)
+        normalise(LAST, [0])
         product_2(LAST - 2)
+        turn_qn_tile(LAST, 0)
+        normalise(LAST, [1])
+        copy_qn_tile(LAST, 0, S)
+        quantise_qn(LAST - 1)
+        turn_qn_tile(LAST, 1)
         copy_nope(LAST - 2)
         copy_rope(LAST - 2, None)
+        copy_qn_tile(LAST, 1, S)
+        quantise_qn_tile(LAST, 0)
         rotate(LAST - 2)
-        turn_qn(LAST)
-        copy_qn(LAST)
-        quantise_qn(LAST)
         product_2(LAST - 1)
+        product_2_tile(LAST, 0)
+        quantise_qn_tile(LAST, 1)
         copy_nope(LAST - 1)
         copy_rope(LAST - 1, None)
         rotate(LAST - 1)
-        product_2(LAST)
-        copy_nope(LAST)
-        copy_rope(LAST, None)
-        rotate(LAST)
+        product_2_tile(LAST, 1)
+        multiply_tile(LAST, 0)
+        copy_nope_of_tile(LAST, 0)
+        multiply_tile(LAST, 1)
+        sum_tile(LAST, 0)
+        copy_nope_of_tile(LAST, 1)
+        sum_tile(LAST, 1)

@@ -32,7 +32,6 @@ ROUNDS = BATCH * SEQ_TILES // ROUND_TILES
 ROUNDS_PER_BATCH = SEQ_TILES // ROUND_TILES
 LAST = ROUNDS - 1
 FREQS_AFTER = 2
-GPSIMD_COLS = 192
 
 PRODUCT_1_LAG = 1
 NORMALISE_LAG = 2
@@ -60,7 +59,6 @@ def tile_mla_pa_t_kernel(
         pair = ctx.enter_context(tc.tile_pool(name="pair", bufs=2))
         ring = ctx.enter_context(tc.tile_pool(name="ring", bufs=3))
         once = ctx.enter_context(tc.tile_pool(name="once", bufs=ROUNDS))
-        early = ctx.enter_context(tc.tile_pool(name="early", bufs=LAST - 3))
         ps_words = ctx.enter_context(tc.psum_pool(name="ps_words", bufs=2))
         ps_ql = ctx.enter_context(tc.psum_pool(name="ps_ql", bufs=3))
         ps_qnt = ctx.enter_context(tc.psum_pool(name="ps_qnt", bufs=1))
@@ -241,7 +239,7 @@ def tile_mla_pa_t_kernel(
                 )
 
         x_banks, x_grouped, x_mx, ql_banks, rstd_of = {}, {}, {}, {}, {}
-        rope_values, products_of = {}, {}
+        products_of = {}
         qn_of, qn_banks, qn_grouped, qn_mx, q_banks = {}, {}, {}, {}, {}
 
         def turn_x(rnd, j):
@@ -488,21 +486,11 @@ def tile_mla_pa_t_kernel(
 
         def copy_rope(rnd, copy):
             rope_bank = q_banks[rnd][1][:].rearrange("p j q -> p (j q)")
-            g_cols = GPSIMD_COLS if copy is not None else 0
-            pool, tag = (early, "products") if g_cols else (ring, "last_products")
-            products_of[rnd] = pool.tile([P, 2, ROUND_TILES * ROPE_COLS], F32, tag=tag, name="products")
-            if g_cols < ROUND_TILES * ROPE_COLS:
-                cols = slice(g_cols, ROUND_TILES * ROPE_COLS)
-                multiply(rnd, nc.vector, rope_bank[:, cols], cols)
-            if g_cols:
-                v = early.tile([P, GPSIMD_COLS], F32, tag="v")
-                copy(out=v[:], in_=rope_bank[:, 0:GPSIMD_COLS])
-                rope_values[rnd] = v
+            products_of[rnd] = once.tile([P, 2, ROUND_TILES * ROPE_COLS], F32, tag="products", name="products")
+            multiply(rnd, nc.vector, rope_bank, slice(0, ROUND_TILES * ROPE_COLS))
 
         def rotate(rnd):
             b, s0 = place(rnd)
-            if rnd in rope_values:
-                multiply(rnd, nc.gpsimd, rope_values[rnd][:], slice(0, GPSIMD_COLS))
             products = products_of[rnd]
             rope = once.tile([P, ROUND_TILES, ROPE_COLS], F32, tag="rope")
             adder = nc.vector if rnd >= LAST - 2 else nc.gpsimd
@@ -556,7 +544,7 @@ def tile_mla_pa_t_kernel(
             run(copy_qn, n - 3)
             run(product_2, n - 4)
             run(lambda r: normalise(r, [1]), n - 2)
-            run(lambda r: copy_rope(r, V if r <= LAST - 4 else None), n - 4)
+            run(lambda r: copy_rope(r, None), n - 4)
             run(copy_nope, n - 4)
             run(quantise_qn, n - 3)
             run(quantise_x, n)

from contextlib import ExitStack

import concourse.mybir as mybir
from concourse.masks import make_identity

F32 = mybir.dt.float32
BF16 = mybir.dt.bfloat16
U32 = mybir.dt.uint32
U8 = mybir.dt.uint8
FP8X4 = mybir.dt.float8_e4m3fn_x4
ACT = mybir.ActivationFunctionType
ALU = mybir.AluOpType

P = 128
PACK = 4
K_PASS = P * PACK

BATCH, SEQ, DIM = 4, 1024, 1024
Q_LORA = 512
HEADS, NOPE, ROPE = 2, 128, 64
EPS = 1e-6

SEQ_TILES = SEQ // P
PASSES_1 = DIM // K_PASS
WORD_BLOCKS = DIM // 2 // P
NOPE_COLS = HEADS * NOPE
ROPE_COLS = HEADS * ROPE
Q_COLS = NOPE_COLS + ROPE_COLS

ROUND_TILES = 2
ROUNDS = BATCH * SEQ_TILES // ROUND_TILES
ROUNDS_PER_BATCH = SEQ_TILES // ROUND_TILES
LAST = ROUNDS - 1
FREQS_AFTER = 2

PRODUCT_1_LAG = 1
NORMALISE_LAG = 2
TURN_QN_LAG = 3
PRODUCT_2_LAG = 4
FINISH_LAG = 5
PREPARE_WQ_B_STEP = 1

FLOPS = 2 * BATCH * SEQ * (DIM * Q_LORA + Q_LORA * HEADS * (NOPE + ROPE))


def tile_mla_pa_t_kernel(
    tc, x, freqs_cos, freqs_sin, wq_a, q_norm_w, wq_b, out_0, out_1
):
    nc = tc.nc

    x_view = x.rearrange("b (p s) k -> b p s k", s=SEQ_TILES)
    nope_view = out_0.rearrange("b (p s) h d -> b p s (h d)", s=SEQ_TILES)
    rope_view = out_1.rearrange("b (p s) h d -> b p s (h d)", s=SEQ_TILES)

    with ExitStack() as ctx:
        ctx.enter_context(tc.manual_schedule())

        keep = ctx.enter_context(tc.tile_pool(name="keep", bufs=1))
        pair = ctx.enter_context(tc.tile_pool(name="pair", bufs=2))
        ring = ctx.enter_context(tc.tile_pool(name="ring", bufs=3))
        once = ctx.enter_context(tc.tile_pool(name="once", bufs=ROUNDS))
        ps_words = ctx.enter_context(tc.psum_pool(name="ps_words", bufs=2))
        ps_ql = ctx.enter_context(tc.psum_pool(name="ps_ql", bufs=3))
        ps_qnt = ctx.enter_context(tc.psum_pool(name="ps_qnt", bufs=1))
        ps_nope = ctx.enter_context(tc.psum_pool(name="ps_nope", bufs=1))
        ps_rope = ctx.enter_context(tc.psum_pool(name="ps_rope", bufs=1))

        x_rows = []
        for rnd in range(ROUNDS):
            x_round = keep.tile([P, ROUND_TILES, DIM], BF16, name="x_round%d" % rnd)
            x_rows.append(x_round)

        def load_x(rnd, tiles=slice(0, ROUND_TILES)):
            b, s0 = rnd // ROUNDS_PER_BATCH, (rnd % ROUNDS_PER_BATCH) * ROUND_TILES
            nc.sync.dma_start(
                out=x_rows[rnd][:, tiles, :],
                in_=x_view[b, :, s0 + tiles.start : s0 + tiles.stop, :],
            )

        wa_rows = keep.tile([P, PACK, DIM], BF16)
        wa_view = wq_a.rearrange("(r t) k -> r t k", t=PACK)

        def load_wq_a(t):
            nc.sync.dma_start(out=wa_rows[:, t, :], in_=wa_view[:, t, :])

        load_x(0, slice(0, 1))
        load_wq_a(0)
        load_wq_a(1)
        load_x(0, slice(1, 2))
        load_wq_a(2)
        load_wq_a(3)
        load_x(1)

        wb_rows = keep.tile([P, HEADS + 1, Q_LORA], BF16)
        wb_heads = wq_b.rearrange("(h d) k -> d h k", h=HEADS)
        nc.sync.dma_start(out=wb_rows[:, 0:HEADS, :], in_=wb_heads[0:NOPE, :, :])
        for h in range(HEADS):
            nc.sync.dma_start(
                out=wb_rows[h * ROPE : (h + 1) * ROPE, HEADS, :],
                in_=wb_heads[NOPE : NOPE + ROPE, h, :],
            )
        freqs_rows = keep.tile([P, 2, SEQ_TILES, ROPE // 2], BF16)
        for rnd in range(2, ROUNDS):
            load_x(rnd)
            if rnd == FREQS_AFTER:
                for c, freqs in enumerate((freqs_cos, freqs_sin)):
                    nc.sync.dma_start(
                        out=freqs_rows[:, c], in_=freqs.rearrange("(p s) f -> p s f", s=SEQ_TILES)
                    )

        gain_row = keep.tile([P, Q_LORA], BF16)
        nc.gpsimd.memset(gain_row[:], 0.0)
        nc.scalar.dma_start(out=gain_row[0:1, :], in_=q_norm_w.rearrange("(o n) -> o n", o=1))

        ident_f32 = keep.tile([P, P], F32)
        make_identity(nc, ident_f32[:])
        ones = keep.tile([P, P], BF16)
        nc.gpsimd.memset(ones[:], 1.0)

        rot = keep.tile([P, 2, SEQ_TILES, 2, HEADS * ROPE // 2], F32)

        def prepare_rotation(c, e, sign):
            nc.gpsimd.tensor_scalar(
                out=rot[:, c, :, e].rearrange("p s (h f) -> p s h f", h=HEADS),
                in0=freqs_rows[:, c].unsqueeze(2).to_broadcast([P, SEQ_TILES, HEADS, ROPE // 2]),
                scalar1=sign,
                scalar2=0.0,
                op0=ALU.mult,
                op1=ALU.add,
            )

        warm = keep.tile([P, 1], F32)
        nc.scalar.activation(out=warm[:], in_=ones[:, 0:1], func=ACT.Abs_reciprocal_sqrt)

        def idle_bank(which, blocks):
            pool, tag = (
                (ps_qnt, "qnt"),
                (ps_nope, "nope_bank"),
                (ps_rope, "rope_bank"),
                (ps_ql, "ql"),
            )[which]
            return pool.tile([P, blocks, P], F32, tag=tag, name="weight_bank")

        def turn_words(bank, word_blocks):
            for slot, block in enumerate(word_blocks):
                nc.tensor.transpose(bank[:, slot, :], block, ident_f32[:])

        def blocks_of_row_words(words):
            return [
                words[:, 2 * P * g + u : 2 * P * (g + 1) : 2]
                for g in range(PASSES_1)
                for u in range(2)
            ]

        wa_codes = keep.tile([P, PASSES_1, Q_LORA], U32, align_bytes=256)
        wa_scales = keep.tile([P, PASSES_1, Q_LORA], U8, align_bytes=256)
        gain = keep.tile([P, Q_LORA], F32)

        wa_grouped = keep.tile([P, PASSES_1 * Q_LORA * PACK], BF16, align_bytes=256)

        def turn_wq_a(v):
            banks = [idle_bank(v * PASSES_1 + g, WORD_BLOCKS) for g in range(PASSES_1)]
            for e in range(2):
                blocks = blocks_of_row_words(wa_rows[:, 2 * v + e, :].bitcast(F32))
                for g in range(PASSES_1):
                    for u in range(2):
                        nc.tensor.transpose(
                            banks[g][:, 2 * e + u, :], blocks[2 * g + u], ident_f32[:]
                        )
            return banks

        def copy_wq_a(v, g, bank, copy):
            cols = slice(v * 2 * P, (v + 1) * 2 * P)
            grouped_words = wa_grouped[:].bitcast(F32).rearrange(
                "p (g n u) -> p g n u", g=PASSES_1, u=2
            )
            copy(
                out=grouped_words[:, g, cols, :].rearrange("p (r e) u -> p r e u", e=2),
                in_=bank[:].rearrange("p (e u) r -> p r e u", u=2),
            )

        def quantise_wq_a(v, g):
            cols = slice(v * 2 * P, (v + 1) * 2 * P)
            first = (g * Q_LORA + v * 2 * P) * PACK
            nc.vector.quantize_mx(
                out=wa_codes[:, g, cols].bitcast(FP8X4),
                scales=wa_scales[:, g, cols],
                in_=wa_grouped[:, first : first + 2 * P * PACK],
            )

        def spread_gain():
            spread = ps_ql.tile([P, Q_LORA], F32, tag="ql")
            nc.tensor.matmul(out=spread[:], lhsT=ones[:], rhs=gain_row[:], start=True, stop=True)
            nc.scalar.copy(
                out=gain[:].rearrange("p (v r e) -> p v r e", v=2, e=2),
                in_=spread[:].rearrange("p (r v e) -> p v r e", v=2, e=2),
            )

        wb_codes = keep.tile([P, Q_COLS], U32, align_bytes=256)
        wb_scales = keep.tile([P, Q_COLS], U8, align_bytes=256)

        wb_grouped = keep.tile([P, Q_COLS * PACK], BF16, align_bytes=256)

        def every_second_word(i):
            words = wb_rows[:, i, :].bitcast(F32).rearrange("r (p u) -> r u p", u=2)
            return [words[:, u, :] for u in range(2)]

        wb_grouped_words = wb_grouped[:].bitcast(F32).rearrange("p (n u) -> p n u", u=2)

        def turn_rotated_rows():
            bank = idle_bank(2, 2)
            turn_words(bank, every_second_word(HEADS))
            nc.scalar.copy(
                out=wb_grouped_words[:, NOPE_COLS : NOPE_COLS + ROPE_COLS, :].rearrange(
                    "p (e m) u -> p e m u", e=2
                ),
                in_=bank[:].rearrange("p u (m e) -> p e m u", e=2),
            )

        def turn_copied_rows():
            bank = idle_bank(1, 2 * HEADS)
            turn_words(bank, every_second_word(0) + every_second_word(1))
            return bank

        def copy_copied_rows(bank):
            nc.vector.tensor_copy(
                out=wb_grouped_words[:, 0:NOPE_COLS, :].rearrange(
                    "p (i r) u -> p i r u", i=HEADS
                ),
                in_=bank[:].rearrange("p (i u) r -> p i r u", u=2),
            )

        def quantise_wq_b(parts):
            for cols in parts:
                nc.vector.quantize_mx(
                    out=wb_codes[:, cols].bitcast(FP8X4),
                    scales=wb_scales[:, cols],
                    in_=wb_grouped[:, cols.start * PACK : cols.stop * PACK],
                )

        x_banks, x_grouped, x_mx, ql_banks, rstd_of = {}, {}, {}, {}, {}
        products_of = {}
        qn_of, qn_banks, qn_grouped, qn_mx, q_banks = {}, {}, {}, {}, {}

        def turn_x(rnd, j):
            if j == 0:
                grouped = pair.tile([P, ROUND_TILES * DIM], BF16, align_bytes=256, tag="x_grouped")
                x_grouped[rnd] = grouped
                x_banks[rnd] = []
            bank = ps_words.tile([P, WORD_BLOCKS, P], F32, tag="words")
            turn_words(bank, blocks_of_row_words(x_rows[rnd][:, j, :].bitcast(F32)))
            x_banks[rnd].append(bank)

        def copy_x(rnd, j, copy):
            grouped_words = x_grouped[rnd][:].bitcast(F32).rearrange(
                "p (j g r u) -> p j g r u", j=ROUND_TILES, g=PASSES_1, u=2
            )
            copy(
                out=grouped_words[:, j],
                in_=x_banks[rnd][j][:].rearrange("p (g u) r -> p g r u", u=2),
            )

        def quantise_x(rnd, tiles=slice(0, ROUND_TILES)):
            if tiles.start == 0:
                codes = ring.tile(
                    [P, ROUND_TILES * PASSES_1 * P], U32, align_bytes=256, tag="x_codes"
                )
                scales = ring.tile(
                    [P, ROUND_TILES * PASSES_1 * P], U8, align_bytes=256, tag="x_scales"
                )
                x_mx[rnd] = (codes, scales)
            codes, scales = x_mx[rnd]
            toks = slice(tiles.start * PASSES_1 * P, tiles.stop * PASSES_1 * P)
            nc.vector.quantize_mx(
                out=codes[:, toks].bitcast(FP8X4),
                scales=scales[:, toks],
                in_=x_grouped[rnd][:, toks.start * PACK : toks.stop * PACK],
            )

        def product_1(rnd, tiles=range(ROUND_TILES)):
            codes, scales = x_mx[rnd]
            if 0 in tiles:
                ql_banks[rnd] = []
            for j in tiles:
                ql = ps_ql.tile([P, Q_LORA], F32, tag="ql")
                for g in range(PASSES_1):
                    tok = slice((j * PASSES_1 + g) * P, (j * PASSES_1 + g + 1) * P)
                    nc.tensor.matmul_mx(
                        out=ql[:],
                        lhsT=codes[:, tok].bitcast(FP8X4),
                        lhsT_scale=scales[:, tok],
                        rhs=wa_codes[:, g, :].bitcast(FP8X4),
                        rhs_scale=wa_scales[:, g, :],
                        start=(g == 0),
                        stop=(g == PASSES_1 - 1),
                    )
                ql_banks[rnd].append(ql)

        def root_mean_square(rnd, tiles=range(ROUND_TILES)):
            if 0 in tiles:
                sum_sq = once.tile([P, ROUND_TILES], F32, tag="sum_sq")
                rstd = once.tile([P, ROUND_TILES], F32, tag="rstd")
                rstd_of[rnd] = (sum_sq, rstd)
            sum_sq, rstd = rstd_of[rnd]
            for j in tiles:
                squares = pair.tile([P, Q_LORA], BF16, tag="squares")
                nc.scalar.activation(
                    out=squares[:],
                    in_=ql_banks[rnd][j][:],
                    func=ACT.Square,
                    accum_out=sum_sq[:, j : j + 1],
                )
                if rnd == LAST:
                    root(rnd, slice(j, j + 1))

        def root(rnd, tiles=slice(0, ROUND_TILES)):
            sum_sq, rstd = rstd_of[rnd]
            nc.scalar.activation(
                out=rstd[:, tiles],
                in_=sum_sq[:, tiles],
                func=ACT.Abs_reciprocal_sqrt,
                bias=EPS,
                scale=1.0 / Q_LORA,
            )

        def normalise(rnd, tiles=range(ROUND_TILES)):
            rstd = rstd_of[rnd][1]
            if 0 in tiles:
                qn_of[rnd] = ring.tile([P, ROUND_TILES, Q_LORA], BF16, tag="qn", name="qn")
            qn = qn_of[rnd]
            for j in tiles:
                nc.vector.scalar_tensor_tensor(
                    out=qn[:, j, :],
                    in0=ql_banks[rnd][j][:],
                    scalar=rstd[:, j : j + 1],
                    in1=gain[:],
                    op0=ALU.mult,
                    op1=ALU.mult,
                )

        def turn_qn_tile(rnd, j):
            pool, tag = ((ps_ql, "ql"), (ps_qnt, "qnt"))[j]
            qnt = pool.tile([P, 2, P], F32, tag=tag, name="qnt")
            words = qn_of[rnd][:, j, :].bitcast(F32)
            turn_words(qnt, [words[:, v * P : (v + 1) * P] for v in range(2)])
            qn_banks[rnd, j] = qnt

        def copy_qn_tile(rnd, j, copy):
            if j == 0:
                qn_grouped[rnd] = pair.tile([P, ROUND_TILES * Q_LORA], BF16, align_bytes=256, tag="qn_grouped", name="grouped")
            copy(
                out=qn_grouped[rnd][:, j * Q_LORA : (j + 1) * Q_LORA].bitcast(F32).rearrange("p (r v) -> p r v", v=2),
                in_=qn_banks[rnd, j][:].rearrange("p v r -> p r v"),
            )

        def quantise_qn_tile(rnd, j):
            if j == 0:
                codes = ring.tile([P, ROUND_TILES * P], U32, align_bytes=256, tag="qn_codes")
                scales = ring.tile([P, ROUND_TILES * P], U8, align_bytes=256, tag="qn_scales")
                qn_mx[rnd] = (codes, scales)
            codes, scales = qn_mx[rnd]
            toks = slice(j * P, (j + 1) * P)
            nc.vector.quantize_mx(
                out=codes[:, toks].bitcast(FP8X4), scales=scales[:, toks],
                in_=qn_grouped[rnd][:, j * Q_LORA : (j + 1) * Q_LORA],
            )

        def product_2_tile(rnd, j):
            codes, scales = qn_mx[rnd]
            rope_bank = ps_ql.tile([P, ROPE_COLS], F32, tag="ql", name="rope_bank")
            pool, tag = ((ps_ql, "ql"), (ps_words, "words"))[j]
            nope_bank = pool.tile([P, NOPE_COLS], F32, tag=tag, name="nope_bank")
            tok = slice(j * P, (j + 1) * P)
            for bank, cols in (
                (rope_bank, slice(NOPE_COLS, Q_COLS)),
                (nope_bank, slice(0, NOPE_COLS)),
            ):
                nc.tensor.matmul_mx(
                    out=bank[:],
                    lhsT=codes[:, tok].bitcast(FP8X4),
                    lhsT_scale=scales[:, tok],
                    rhs=wb_codes[:, cols].bitcast(FP8X4),
                    rhs_scale=wb_scales[:, cols],
                    start=True,
                    stop=True,
                )
            q_banks[rnd, j] = (nope_bank, rope_bank)

        def copy_nope_of_tile(rnd, j):
            b, s0 = place(rnd)
            nope = once.tile([P, NOPE_COLS], F32, tag="nope_tile%d" % j, name="nope_tile", bufs=1)
            nc.scalar.copy(out=nope[:], in_=q_banks[rnd, j][0][:])
            nc.sync.dma_start(out=nope_view[b, :, s0 + j, :], in_=nope[:])

        def multiply_tile(rnd, j):
            s0 = place(rnd)[1]
            products = once.tile([P, 2, ROPE_COLS], F32, tag="products_tile%d" % j, name="products_tile", bufs=1)
            nc.vector.tensor_tensor(
                out=products[:],
                in0=q_banks[rnd, j][1][:].unsqueeze(1).to_broadcast([P, 2, ROPE_COLS]),
                in1=rot[:, :, s0 + j].rearrange("p c e q -> p c (e q)"),
                op=ALU.mult,
            )
            products_of[rnd, j] = products

        def sum_tile(rnd, j):
            b, s0 = place(rnd)
            rope = once.tile([P, ROPE_COLS], F32, tag="rope_tile%d" % j, name="rope_tile", bufs=1)
            by_value = products_of[rnd, j][:].rearrange("p c (e m) -> p c e m", e=2)
            nc.vector.tensor_tensor(
                out=rope[:].rearrange("p (m e) -> p e m", e=2),
                in0=by_value[:, 0],
                in1=by_value[:, 1, ::-1, :],
                op=ALU.add,
            )
            nc.sync.dma_start(out=rope_view[b, :, s0 + j, :], in_=rope[:])

        def turn_qn(rnd):
            qnt = ps_qnt.tile([P, ROUND_TILES * 2, P], F32, tag="qnt")
            blocks = []
            for j in range(ROUND_TILES):
                words = qn_of[rnd][:, j, :].bitcast(F32)
                blocks += [words[:, v * P : (v + 1) * P] for v in range(2)]
            turn_words(qnt, blocks)
            qn_banks[rnd] = qnt

        def copy_qn(rnd):
            grouped = pair.tile([P, ROUND_TILES * Q_LORA], BF16, align_bytes=256, tag="qn_grouped")
            nc.scalar.copy(
                out=grouped[:].bitcast(F32).rearrange("p (j r v) -> p j r v", j=ROUND_TILES, v=2),
                in_=qn_banks[rnd][:].rearrange("p (j v) r -> p j r v", v=2),
            )
            qn_grouped[rnd] = grouped

        def quantise_qn(rnd):
            codes = ring.tile([P, ROUND_TILES * P], U32, align_bytes=256, tag="qn_codes")
            scales = ring.tile([P, ROUND_TILES * P], U8, align_bytes=256, tag="qn_scales")
            nc.vector.quantize_mx(
                out=codes[:].bitcast(FP8X4), scales=scales[:], in_=qn_grouped[rnd][:]
            )
            qn_mx[rnd] = (codes, scales)

        def product_2(rnd):
            codes, scales = qn_mx[rnd]
            spare = {LAST - 2: (ps_words, "words"), LAST: (ps_ql, "ql")}
            pool, tag = spare.get(rnd, (ps_nope, "nope_bank"))
            nope_bank = pool.tile([P, ROUND_TILES, NOPE_COLS], F32, tag=tag, name="nope_bank")
            pool, tag = spare.get(rnd, (ps_rope, "rope_bank"))
            rope_bank = pool.tile([P, ROUND_TILES, ROPE_COLS], F32, tag=tag, name="rope_bank")
            for bank, cols in (
                (rope_bank, slice(NOPE_COLS, Q_COLS)),
                (nope_bank, slice(0, NOPE_COLS)),
            ):
                for j in range(ROUND_TILES):
                    tok = slice(j * P, (j + 1) * P)
                    nc.tensor.matmul_mx(
                        out=bank[:, j, :],
                        lhsT=codes[:, tok].bitcast(FP8X4),
                        lhsT_scale=scales[:, tok],
                        rhs=wb_codes[:, cols].bitcast(FP8X4),
                        rhs_scale=wb_scales[:, cols],
                        start=True,
                        stop=True,
                    )
            q_banks[rnd] = (nope_bank, rope_bank)

        def place(rnd):
            return rnd // ROUNDS_PER_BATCH, (rnd % ROUNDS_PER_BATCH) * ROUND_TILES

        def copy_nope(rnd):
            b, s0 = place(rnd)
            nope = once.tile([P, ROUND_TILES, NOPE_COLS], F32, tag="nope")
            nc.scalar.copy(out=nope[:], in_=q_banks[rnd][0][:])
            nc.sync.dma_start(out=nope_view[b, :, s0 : s0 + ROUND_TILES, :], in_=nope[:])

        def multiply(rnd, engine, values, cols):
            s0 = place(rnd)[1]
            factors = rot[:, :, s0 : s0 + ROUND_TILES].rearrange("p c s e q -> p c (s e q)")
            n = cols.stop - cols.start
            engine.tensor_tensor(
                out=products_of[rnd][:, :, cols],
                in0=values.unsqueeze(1).to_broadcast([P, 2, n]),
                in1=factors[:, :, cols],
                op=ALU.mult,
            )

        def copy_rope(rnd, copy):
            rope_bank = q_banks[rnd][1][:].rearrange("p j q -> p (j q)")
            products_of[rnd] = once.tile([P, 2, ROUND_TILES * ROPE_COLS], F32, tag="products", name="products")
            multiply(rnd, nc.vector, rope_bank, slice(0, ROUND_TILES * ROPE_COLS))

        def rotate(rnd):
            b, s0 = place(rnd)
            products = products_of[rnd]
            rope = once.tile([P, ROUND_TILES, ROPE_COLS], F32, tag="rope")
            adder = nc.vector if rnd >= LAST - 2 else nc.gpsimd
            by_value = products[:].rearrange("p c (j e m) -> p c j e m", e=2, j=ROUND_TILES)
            adder.tensor_tensor(
                out=rope[:].rearrange("p j (m e) -> p j e m", e=2),
                in0=by_value[:, 0],
                in1=by_value[:, 1, :, ::-1, :],
                op=ALU.add,
            )
            nc.sync.dma_start(out=rope_view[b, :, s0 : s0 + ROUND_TILES, :], in_=rope[:])

        def run(stage_of_round, rnd):
            if 0 <= rnd < ROUNDS:
                stage_of_round(rnd)

        turn_x(0, 0)
        copy_x(0, 0, nc.vector.tensor_copy)
        quantise_x(0, slice(0, 1))
        banks = turn_wq_a(0)
        copy_wq_a(0, 0, banks[0], nc.scalar.copy)
        copy_wq_a(0, 1, banks[1], nc.vector.tensor_copy)
        turn_x(0, 1)
        copy_x(0, 1, nc.scalar.copy)
        quantise_wq_a(0, 0)
        quantise_wq_a(0, 1)
        quantise_x(0, slice(1, 2))
        banks = turn_wq_a(1)
        copy_wq_a(1, 0, banks[0], nc.scalar.copy)
        copy_wq_a(1, 1, banks[1], nc.vector.tensor_copy)
        quantise_wq_a(1, 0)
        quantise_wq_a(1, 1)
        spread_gain()

        S, V = nc.scalar.copy, nc.vector.tensor_copy
        for e, sign in enumerate((1.0, -1.0)):
            prepare_rotation(0, e, 1.0)
            prepare_rotation(1, e, sign)
        for step in range(1, ROUNDS + 1):
            n = step
            run(lambda r: root(r, slice(0, 1)), n - 2)
            if n < ROUNDS:
                turn_x(n, 0)
                copy_x(n, 0, S)
                turn_x(n, 1)
            run(lambda r: root(r, slice(1, 2)), n - 2)
            run(lambda r: normalise(r, [0]), n - 2)
            if n < ROUNDS:
                copy_x(n, 1, V)
            run(turn_qn, n - 3)
            run(copy_qn, n - 3)
            run(product_2, n - 4)
            run(lambda r: normalise(r, [1]), n - 2)
            run(lambda r: copy_rope(r, None), n - 4)
            run(copy_nope, n - 4)
            run(quantise_qn, n - 3)
            run(quantise_x, n)
            if n == 2:
                quantise_wq_b([slice(0, NOPE_COLS)])
            if n == 3:
                quantise_wq_b([slice(NOPE_COLS, Q_COLS)])
            run(rotate, n - 4)
            run(product_1, n - 1)
            if n == 1:
                wb_bank = turn_copied_rows()
            run(root_mean_square, n - 1)
            if n == 1:
                copy_copied_rows(wb_bank)
            if n == 2:
                turn_rotated_rows()
        turn_qn(LAST - 1)
        copy_qn(LAST - 1)
        normalise(LAST, [0])
        product_2(LAST - 2)
        turn_qn_tile(LAST, 0)
        normalise(LAST, [1])
        copy_qn_tile(LAST, 0, S)
        quantise_qn(LAST - 1)
        turn_qn_tile(LAST, 1)
        copy_nope(LAST - 2)
        copy_rope(LAST - 2, None)
        copy_qn_tile(LAST, 1, S)
        quantise_qn_tile(LAST, 0)
        rotate(LAST - 2)
        product_2(LAST - 1)
        product_2_tile(LAST, 0)
        quantise_qn_tile(LAST, 1)
        copy_nope(LAST - 1)
        copy_rope(LAST - 1, None)
        rotate(LAST - 1)
        product_2_tile(LAST, 1)
        multiply_tile(LAST, 0)
        copy_nope_of_tile(LAST, 0)
        multiply_tile(LAST, 1)
        sum_tile(LAST, 0)
        copy_nope_of_tile(LAST, 1)
        sum_tile(LAST, 1)
